import numpy as np
import ml_dtypes


def mxq(x, axis, fmt="e4m3"):
    dtype, down = {"e4m3": (ml_dtypes.float8_e4m3fn, 7), "e5m2": (ml_dtypes.float8_e5m2, 14)}[fmt]
    v = np.moveaxis(np.asarray(x, np.float32).astype(ml_dtypes.bfloat16).astype(np.float64), axis, -1)
    blocks = v.reshape(v.shape[:-1] + (-1, 32))
    amax = np.abs(blocks).max(-1, keepdims=True)
    byte = np.maximum(np.where(amax > 0, np.frexp(amax)[1] - 1 + 127, 0) - down, 1)
    scale = np.exp2(byte - 127.0)
    codes = (blocks / scale).astype(np.float32).astype(dtype).astype(np.float64)
    return np.moveaxis((codes * scale).reshape(v.shape), -1, axis)


WIDE = False


def mx_kscale(k):
    if not WIDE:
        return np.ones(k)
    levels = np.array([10, -10, 5, -5, 0])
    a = np.random.permutation(np.resize(levels, k // 512 * 4)).reshape(k // 512, 4)
    idx = np.arange(k)
    return np.exp2(a[idx // 512, idx % 128 // 32])


BF16 = ml_dtypes.bfloat16


def bf(x):
    return np.asarray(x, np.float32).astype(BF16)


def f64(x):
    return np.asarray(x).astype(np.float64)


B, SEQ, C, P, H, W = 2, 8, 1024, 512, 8, 8
L = SEQ * H * W


def setup_inputs():
    s = mx_kscale(P)
    return {"att_logits": bf(np.random.standard_normal((B, L, L)) * 2.0),
            "g": bf(np.random.standard_normal((B, P, L)) * s[None, :, None]),
            "w1_w": bf(np.random.standard_normal((C, P)) / np.sqrt(P) / s[None, :]),
            "w1_b": bf(np.random.standard_normal(C) * 0.1),
            "w2_w": bf(np.random.standard_normal((C, P)) * 2.0 / np.sqrt(P) / s[None, :]),
            "w2_b": bf(np.random.standard_normal(C) * 0.1)}


def reference(att_logits, g, w1_w, w1_b, w2_w, w2_b):
    a = f64(att_logits)
    gg = f64(g)
    e = np.exp(a - a.max(-1, keepdims=True))
    y = (mxq(e, 2, "e4m3") @ mxq(gg, 2, "e4m3").transpose(0, 2, 1)) / e.sum(-1, keepdims=True)
    x2 = (mxq(y, 2, "e4m3") @ mxq(f64(w2_w), 1, "e4m3").T) + f64(w2_b)
    x1 = (mxq(gg, 1, "e4m3").transpose(0, 2, 1) @ mxq(f64(w1_w), 1, "e4m3").T) + f64(w1_b)
    return (x1 + x2).transpose(0, 2, 1)

@@ -1,0 +1,236 @@
+from contextlib import ExitStack
+
+import concourse.masks as masks
+import concourse.mybir as mybir
+
+BF16 = mybir.dt.bfloat16
+F32 = mybir.dt.float32
+U32 = mybir.dt.uint32
+U8 = mybir.dt.uint8
+FP8X4 = mybir.dt.float8_e4m3fn_x4
+ACT = mybir.ActivationFunctionType
+ALU = mybir.AluOpType
+AXIS = mybir.AxisListType
+
+CLIPS = 2
+POSITIONS = 512
+FEATURES = 512
+CHANNELS = 1024
+
+PART = 128
+PACK = 4
+K_PASS = PART * PACK
+L_TILES = POSITIONS // PART
+P_TILES = FEATURES // PART
+C_TILES = CHANNELS // PART
+
+FLOPS = 2 * CLIPS * (POSITIONS * POSITIONS * FEATURES + 2 * POSITIONS * FEATURES * CHANNELS)
+
+
+def cols(i, width):
+    return slice(i * width, (i + 1) * width)
+
+
+def tile_stnonlocalgnlstage_pb_kernel(tc, att_logits, g, w1_w, w1_b, w2_w, w2_b, out):
+    nc = tc.nc
+    with ExitStack() as ctx:
+        const = ctx.enter_context(tc.tile_pool(name="const", bufs=1))
+        per_weight = ctx.enter_context(tc.tile_pool(name="per_weight", bufs=2))
+        per_clip = ctx.enter_context(tc.tile_pool(name="per_clip", bufs=CLIPS))
+        psum_t = ctx.enter_context(tc.psum_pool(name="psum_t", bufs=3))
+        psum_y = ctx.enter_context(tc.psum_pool(name="psum_y", bufs=2))
+        psum_o = ctx.enter_context(tc.psum_pool(name="psum_o", bufs=3))
+
+        ident_f32 = const.tile([PART, PART], F32)
+        masks.make_identity(nc, ident_f32[:])
+        ident_bf16 = const.tile([PART, PART], BF16)
+        masks.make_identity(nc, ident_bf16[:])
+
+        warm = const.tile([PART, 1], F32)
+        nc.vector.memset(warm[:], 0.0)
+        nc.scalar.activation(out=warm[:], in_=warm[:], func=ACT.Exp)
+
+        def load_clip(b):
+            att_rows = per_clip.tile([PART, L_TILES, POSITIONS], BF16)
+            nc.sync.dma_start(out=att_rows[:], in_=att_logits[b].rearrange("(lt l) m -> l lt m", l=PART))
+            g_rows = per_clip.tile([PART, PACK * POSITIONS], BF16)
+            nc.sync.dma_start(
+                out=g_rows[:].rearrange("j (u e m) -> j u e m", u=2, e=2),
+                in_=g[b].rearrange("(u j e) m -> j u e m", u=2, e=2),
+            )
+            return att_rows, g_rows
+
+        def load_weight(w):
+            w_rows = per_weight.tile([PART, C_TILES * FEATURES], BF16)
+            nc.sync.dma_start(out=w_rows[:], in_=w.rearrange("(i ct) p -> i (ct p)", ct=C_TILES))
+            return w_rows
+
+        att_rows_0, g_rows_0 = load_clip(0)
+        w1_rows = load_weight(w1_w)
+        w2_rows = load_weight(w2_w)
+        att_rows_1, g_rows_1 = load_clip(1)
+        att_rows = [att_rows_0, att_rows_1]
+        g_rows = [g_rows_0, g_rows_1]
+
+        b1 = const.tile([PART, C_TILES], BF16)
+        nc.scalar.dma_start(out=b1[:], in_=w1_b.rearrange("(i ct) -> i ct", ct=C_TILES))
+        b2 = const.tile([PART, C_TILES], BF16)
+        nc.scalar.dma_start(out=b2[:], in_=w2_b.rearrange("(i ct) -> i ct", ct=C_TILES))
+        bias = const.tile([PART, C_TILES], F32)
+        nc.vector.tensor_tensor(out=bias[:], in0=b1[:], in1=b2[:], op=ALU.add)
+
+        def transpose_words(rows, grouped, n_tiles, copy):
+            words = rows[:].bitcast(F32)
+            grouped_words = grouped[:].bitcast(F32)
+            for pair in range(n_tiles // 2):
+                bank = psum_t.tile([PART, 2, 2, PART], F32, tag="t")
+                for n in range(2):
+                    for u in range(2):
+                        nc.tensor.transpose(bank[:, n, u, :], words[:, cols(4 * pair + 2 * n + u, PART)], ident_f32[:])
+                copy(
+                    out=grouped_words[:, cols(pair, 4 * PART)].rearrange("q (n r u) -> q n r u", n=2, u=2),
+                    in_=bank[:].rearrange("q n u r -> q n r u"),
+                )
+
+        def quantise(grouped, codes, scales, piece, width):
+            nc.vector.quantize_mx(
+                out=codes[:, cols(piece, width)].bitcast(FP8X4),
+                scales=scales[:, cols(piece, width)],
+                in_=grouped[:, cols(piece, PACK * width)],
+            )
+
+        def prepare_weight(w_rows):
+            w_grouped = per_weight.tile([PART, CHANNELS * PACK], BF16, align_bytes=64)
+            w_codes = per_weight.tile([PART, CHANNELS], U32, align_bytes=64)
+            w_scales = per_weight.tile([PART, CHANNELS], U8, align_bytes=64)
+            transpose_words(w_rows, w_grouped, C_TILES, nc.scalar.copy)
+            quantise(w_grouped, w_codes, w_scales, 0, CHANNELS)
+            return w_codes, w_scales
+
+        def softmax_numerator(b):
+            neg_max = per_clip.tile([PART, L_TILES], F32)
+            e_sum = per_clip.tile([PART, L_TILES], F32)
+            e_rows = per_clip.tile([PART, L_TILES, PACK, PART], BF16)
+            for lt in range(L_TILES):
+                nc.vector.tensor_reduce(
+                    out=neg_max[:, lt : lt + 1], in_=att_rows[b][:, lt, :], axis=AXIS.X, op=ALU.max, negate=True
+                )
+                nc.scalar.activation(
+                    out=e_rows[:, lt, :, :].rearrange("l (u e) q -> l u e q", u=2),
+                    in_=att_rows[b][:, lt, :].rearrange("l (u q e) -> l u e q", u=2, e=2),
+                    func=ACT.Exp,
+                    bias=neg_max[:, lt : lt + 1],
+                    scale=1.0,
+                    accum_out=e_sum[:, lt : lt + 1],
+                )
+            return e_rows, e_sum
+
+        def prepare_g(b):
+            gm_grouped = per_clip.tile([PART, FEATURES * PACK], BF16, align_bytes=64)
+            gm_codes = per_clip.tile([PART, FEATURES], U32, align_bytes=64)
+            gm_scales = per_clip.tile([PART, FEATURES], U8, align_bytes=64)
+            transpose_words(g_rows[b], gm_grouped, P_TILES, nc.vector.tensor_copy)
+            gp_grouped = per_clip.tile([PART, POSITIONS * PACK], BF16, align_bytes=64)
+            gp_codes = per_clip.tile([PART, POSITIONS], U32, align_bytes=64)
+            gp_scales = per_clip.tile([PART, POSITIONS], U8, align_bytes=64)
+            nc.vector.tensor_copy(
+                out=gp_grouped[:].rearrange("q (c i t) -> q c t i", i=4, t=PACK),
+                in_=g_rows[b][:].rearrange("q (t c i) -> q c t i", t=PACK, i=4),
+            )
+            quantise(gm_grouped, gm_codes, gm_scales, 0, FEATURES)
+            quantise(gp_grouped, gp_codes, gp_scales, 0, POSITIONS)
+            return gm_codes, gm_scales, gp_codes, gp_scales
+
+        def prepare_e(e_rows, e_sum):
+            e_grouped = per_clip.tile([PART, POSITIONS * PACK], BF16, align_bytes=64)
+            e_codes = per_clip.tile([PART, POSITIONS], U32, align_bytes=64)
+            e_scales = per_clip.tile([PART, POSITIONS], U8, align_bytes=64)
+            for lt in range(L_TILES):
+                bank = psum_t.tile([PART, PACK, PART], BF16, tag="t")
+                for t in range(PACK):
+                    nc.tensor.transpose(bank[:, t, :], e_rows[:, lt, t, :], ident_bf16[:])
+                nc.scalar.copy(
+                    out=e_grouped[:, cols(lt, PACK * PART)].rearrange("q (l t) -> q l t", t=PACK),
+                    in_=bank[:].rearrange("q t l -> q l t"),
+                )
+                quantise(e_grouped, e_codes, e_scales, lt, PART)
+            e_recip = per_clip.tile([PART, L_TILES], F32)
+            nc.vector.reciprocal(out=e_recip[:], in_=e_sum[:])
+            bank = psum_t.tile([PART, POSITIONS], F32, tag="t")
+            for lt in range(L_TILES):
+                nc.tensor.transpose(
+                    bank[:, cols(lt, PART)], e_recip[:, lt : lt + 1].to_broadcast([PART, PART]), ident_f32[:]
+                )
+            recip_rows = per_clip.tile([PART, POSITIONS], F32)
+            nc.scalar.copy(out=recip_rows[:], in_=bank[:])
+            return e_codes, e_scales, recip_rows
+
+        def aggregate(e_codes, e_scales, gm_codes, gm_scales, recip_rows):
+            y_grouped = per_clip.tile([PART, POSITIONS * PACK], BF16, align_bytes=64)
+            y_codes = per_clip.tile([PART, POSITIONS], U32, align_bytes=64)
+            y_scales = per_clip.tile([PART, POSITIONS], U8, align_bytes=64)
+            for lt in range(L_TILES):
+                bank = psum_y.tile([PART, PACK, PART], F32)
+                for t in range(PACK):
+                    nc.tensor.matmul_mx(
+                        out=bank[:, t, :],
+                        lhsT=gm_codes[:, cols(t, PART)].bitcast(FP8X4),
+                        lhsT_scale=gm_scales[:, cols(t, PART)],
+                        rhs=e_codes[:, cols(lt, PART)].bitcast(FP8X4),
+                        rhs_scale=e_scales[:, cols(lt, PART)],
+                        start=True,
+                        stop=True,
+                    )
+                nc.vector.tensor_tensor(
+                    out=y_grouped[:, cols(lt, PACK * PART)].rearrange("q (l t) -> q l t", t=PACK),
+                    in0=bank[:].rearrange("q t l -> q l t"),
+                    in1=recip_rows[:, cols(lt, PART)].unsqueeze(2).to_broadcast([PART, PART, PACK]),
+                    op=ALU.mult,
+                )
+                quantise(y_grouped, y_codes, y_scales, lt, PART)
+            return y_codes, y_scales
+
+        def project(b, gp_codes, gp_scales, y_codes, y_scales):
+            result = per_clip.tile([PART, C_TILES, POSITIONS], F32)
+            out_rows = out[b].rearrange("(i ct) l -> i ct l", ct=C_TILES)
+            for ct in range(C_TILES):
+                bank = psum_o.tile([PART, POSITIONS], F32)
+                nc.tensor.matmul_mx(
+                    out=bank[:],
+                    lhsT=w1_codes[:, cols(ct, PART)].bitcast(FP8X4),
+                    lhsT_scale=w1_scales[:, cols(ct, PART)],
+                    rhs=gp_codes[:].bitcast(FP8X4),
+                    rhs_scale=gp_scales[:],
+                    start=True,
+                    stop=False,
+                )
+                nc.tensor.matmul_mx(
+                    out=bank[:],
+                    lhsT=w2_codes[:, cols(ct, PART)].bitcast(FP8X4),
+                    lhsT_scale=w2_scales[:, cols(ct, PART)],
+                    rhs=y_codes[:].bitcast(FP8X4),
+                    rhs_scale=y_scales[:],
+                    start=False,
+                    stop=True,
+                )
+                if ct % 3 == 2:
+                    nc.vector.tensor_scalar_add(out=result[:, ct, :], in0=bank[:], scalar1=bias[:, ct : ct + 1])
+                else:
+                    nc.scalar.activation(
+                        out=result[:, ct, :], in_=bank[:], func=ACT.Identity, bias=bias[:, ct : ct + 1], scale=1.0
+                    )
+                if ct % 2 == 1:
+                    nc.sync.dma_start(out=out_rows[:, ct - 1 : ct + 1, :], in_=result[:, ct - 1 : ct + 1, :])
+
+        e_rows_0, e_sum_0 = softmax_numerator(0)
+        gm_codes_0, gm_scales_0, gp_codes_0, gp_scales_0 = prepare_g(0)
+        e_codes_0, e_scales_0, recip_rows_0 = prepare_e(e_rows_0, e_sum_0)
+        w1_codes, w1_scales = prepare_weight(w1_rows)
+        y_codes_0, y_scales_0 = aggregate(e_codes_0, e_scales_0, gm_codes_0, gm_scales_0, recip_rows_0)
+        w2_codes, w2_scales = prepare_weight(w2_rows)
+        e_rows_1, e_sum_1 = softmax_numerator(1)
+        project(0, gp_codes_0, gp_scales_0, y_codes_0, y_scales_0)
+        gm_codes_1, gm_scales_1, gp_codes_1, gp_scales_1 = prepare_g(1)
+        e_codes_1, e_scales_1, recip_rows_1 = prepare_e(e_rows_1, e_sum_1)
+        y_codes_1, y_scales_1 = aggregate(e_codes_1, e_scales_1, gm_codes_1, gm_scales_1, recip_rows_1)
+        project(1, gp_codes_1, gp_scales_1, y_codes_1, y_scales_1)

@@ -19,10 +19,10 @@ CHANNELS = 1024
 
 PART = 128
 PACK = 4
-K_PASS = PART * PACK
 L_TILES = POSITIONS // PART
 P_TILES = FEATURES // PART
 C_TILES = CHANNELS // PART
+PSUM_BANKS = 8
 
 FLOPS = 2 * CLIPS * (POSITIONS * POSITIONS * FEATURES + 2 * POSITIONS * FEATURES * CHANNELS)
 
@@ -34,203 +34,213 @@ def cols(i, width):
 def tile_stnonlocalgnlstage_pb_kernel(tc, att_logits, g, w1_w, w1_b, w2_w, w2_b, out):
     nc = tc.nc
     with ExitStack() as ctx:
-        const = ctx.enter_context(tc.tile_pool(name="const", bufs=1))
-        per_weight = ctx.enter_context(tc.tile_pool(name="per_weight", bufs=2))
-        per_clip = ctx.enter_context(tc.tile_pool(name="per_clip", bufs=CLIPS))
-        psum_t = ctx.enter_context(tc.psum_pool(name="psum_t", bufs=3))
-        psum_y = ctx.enter_context(tc.psum_pool(name="psum_y", bufs=2))
-        psum_o = ctx.enter_context(tc.psum_pool(name="psum_o", bufs=3))
+        sbuf = ctx.enter_context(tc.tile_pool(name="sbuf", bufs=1))
+        psum = ctx.enter_context(tc.psum_pool(name="psum", bufs=PSUM_BANKS))
+        ctx.enter_context(tc.manual_schedule())
 
-        ident_f32 = const.tile([PART, PART], F32)
+        def bank(shape, dtype):
+            return psum.tile(shape, dtype, name="bank", tag="bank")
+
+        def mx_operand(name, n_cols):
+            return {
+                "values": sbuf.tile([PART, n_cols * PACK], BF16, name=name + "_values", align_bytes=64),
+                "codes": sbuf.tile([PART, n_cols], U32, name=name + "_codes", align_bytes=64),
+                "scales": sbuf.tile([PART, n_cols], U8, name=name + "_scales", align_bytes=64),
+            }
+
+        def quantise(operand, piece, width):
+            nc.vector.quantize_mx(
+                out=operand["codes"][:, cols(piece, width)].bitcast(FP8X4),
+                scales=operand["scales"][:, cols(piece, width)],
+                in_=operand["values"][:, cols(piece, PACK * width)],
+            )
+
+        def multiply(acc, stationary, s_piece, moving, m_piece, m_width, start, stop):
+            nc.tensor.matmul_mx(
+                out=acc,
+                lhsT=stationary["codes"][:, cols(s_piece, PART)].bitcast(FP8X4),
+                lhsT_scale=stationary["scales"][:, cols(s_piece, PART)],
+                rhs=moving["codes"][:, cols(m_piece, m_width)].bitcast(FP8X4),
+                rhs_scale=moving["scales"][:, cols(m_piece, m_width)],
+                start=start,
+                stop=stop,
+            )
+
+        ident_f32 = sbuf.tile([PART, PART], F32)
         masks.make_identity(nc, ident_f32[:])
-        ident_bf16 = const.tile([PART, PART], BF16)
+        ident_bf16 = sbuf.tile([PART, PART], BF16)
         masks.make_identity(nc, ident_bf16[:])
 
-        warm = const.tile([PART, 1], F32)
+        warm = sbuf.tile([PART, 1], F32)
         nc.vector.memset(warm[:], 0.0)
         nc.scalar.activation(out=warm[:], in_=warm[:], func=ACT.Exp)
 
-        def load_clip(b):
-            att_rows = per_clip.tile([PART, L_TILES, POSITIONS], BF16)
-            nc.sync.dma_start(out=att_rows[:], in_=att_logits[b].rearrange("(lt l) m -> l lt m", l=PART))
-            g_rows = per_clip.tile([PART, PACK * POSITIONS], BF16)
+        att_rows = [sbuf.tile([PART, L_TILES, POSITIONS], BF16, name="att_rows%d" % b) for b in range(CLIPS)]
+        g_rows = [sbuf.tile([PART, PACK * POSITIONS], BF16, name="g_rows%d" % b) for b in range(CLIPS)]
+        w_rows = [sbuf.tile([PART, C_TILES * FEATURES], BF16, name="w_rows%d" % i) for i in range(2)]
+        b1 = sbuf.tile([PART, C_TILES], BF16)
+        b2 = sbuf.tile([PART, C_TILES], BF16)
+        bias = sbuf.tile([PART, C_TILES], F32)
+        neg_max = [sbuf.tile([PART, L_TILES], F32, name="neg_max%d" % b) for b in range(CLIPS)]
+        e_sum = [sbuf.tile([PART, L_TILES], F32, name="e_sum%d" % b) for b in range(CLIPS)]
+        e_recip = [sbuf.tile([PART, L_TILES], F32, name="e_recip%d" % b) for b in range(CLIPS)]
+        e_rows = [sbuf.tile([PART, L_TILES, PACK, PART], BF16, name="e_rows%d" % b) for b in range(CLIPS)]
+        recip_rows = [sbuf.tile([PART, POSITIONS], F32, name="recip_rows%d" % b) for b in range(CLIPS)]
+        result = [sbuf.tile([PART, C_TILES, POSITIONS], F32, name="result%d" % b) for b in range(CLIPS)]
+        e_by_m = [mx_operand("e_by_m%d" % b, POSITIONS) for b in range(CLIPS)]
+        g_by_m = [mx_operand("g_by_m%d" % b, FEATURES) for b in range(CLIPS)]
+        g_by_p = [mx_operand("g_by_p%d" % b, POSITIONS) for b in range(CLIPS)]
+        y_by_p = [mx_operand("y_by_p%d" % b, POSITIONS) for b in range(CLIPS)]
+        w_by_p = [mx_operand("w_by_p%d" % i, CHANNELS) for i in range(2)]
+
+        def load_g(b):
             nc.sync.dma_start(
-                out=g_rows[:].rearrange("j (u e m) -> j u e m", u=2, e=2),
+                out=g_rows[b][:].rearrange("j (u e m) -> j u e m", u=2, e=2),
                 in_=g[b].rearrange("(u j e) m -> j u e m", u=2, e=2),
             )
-            return att_rows, g_rows
 
-        def load_weight(w):
-            w_rows = per_weight.tile([PART, C_TILES * FEATURES], BF16)
-            nc.sync.dma_start(out=w_rows[:], in_=w.rearrange("(i ct) p -> i (ct p)", ct=C_TILES))
-            return w_rows
+        def load_w(i, w):
+            nc.sync.dma_start(out=w_rows[i][:], in_=w.rearrange("(i ct) p -> i (ct p)", ct=C_TILES))
 
-        att_rows_0, g_rows_0 = load_clip(0)
-        w1_rows = load_weight(w1_w)
-        w2_rows = load_weight(w2_w)
-        att_rows_1, g_rows_1 = load_clip(1)
-        att_rows = [att_rows_0, att_rows_1]
-        g_rows = [g_rows_0, g_rows_1]
+        for lt in range(L_TILES):
+            nc.sync.dma_start(out=att_rows[0][:, lt, :], in_=att_logits[0, cols(lt, PART), :])
+        load_g(0)
+        load_w(0, w1_w)
+        load_w(1, w2_w)
+        nc.sync.dma_start(out=att_rows[1][:], in_=att_logits[1].rearrange("(lt l) m -> l lt m", l=PART))
+        load_g(1)
+        nc.sync.dma_start(out=b1[:], in_=w1_b.rearrange("(i ct) -> i ct", ct=C_TILES))
+        nc.sync.dma_start(out=b2[:], in_=w2_b.rearrange("(i ct) -> i ct", ct=C_TILES))
 
-        b1 = const.tile([PART, C_TILES], BF16)
-        nc.scalar.dma_start(out=b1[:], in_=w1_b.rearrange("(i ct) -> i ct", ct=C_TILES))
-        b2 = const.tile([PART, C_TILES], BF16)
-        nc.scalar.dma_start(out=b2[:], in_=w2_b.rearrange("(i ct) -> i ct", ct=C_TILES))
-        bias = const.tile([PART, C_TILES], F32)
-        nc.vector.tensor_tensor(out=bias[:], in0=b1[:], in1=b2[:], op=ALU.add)
-
-        def transpose_words(rows, grouped, n_tiles, copy):
+        def transpose_words(rows, operand, n_blocks, copy):
             words = rows[:].bitcast(F32)
-            grouped_words = grouped[:].bitcast(F32)
-            for pair in range(n_tiles // 2):
-                bank = psum_t.tile([PART, 2, 2, PART], F32, tag="t")
+            value_words = operand["values"][:].bitcast(F32)
+            for pair in range(n_blocks // 2):
+                acc = bank([PART, 2, 2, PART], F32)
                 for n in range(2):
                     for u in range(2):
-                        nc.tensor.transpose(bank[:, n, u, :], words[:, cols(4 * pair + 2 * n + u, PART)], ident_f32[:])
+                        nc.tensor.transpose(acc[:, n, u, :], words[:, cols(4 * pair + 2 * n + u, PART)], ident_f32[:])
                 copy(
-                    out=grouped_words[:, cols(pair, 4 * PART)].rearrange("q (n r u) -> q n r u", n=2, u=2),
-                    in_=bank[:].rearrange("q n u r -> q n r u"),
+                    out=value_words[:, cols(pair, 4 * PART)].rearrange("q (n r u) -> q n r u", n=2, u=2),
+                    in_=acc[:].rearrange("q n u r -> q n r u"),
                 )
 
-        def quantise(grouped, codes, scales, piece, width):
-            nc.vector.quantize_mx(
-                out=codes[:, cols(piece, width)].bitcast(FP8X4),
-                scales=scales[:, cols(piece, width)],
-                in_=grouped[:, cols(piece, PACK * width)],
+        def row_max(b, lt):
+            nc.vector.tensor_reduce(
+                out=neg_max[b][:, lt : lt + 1], in_=att_rows[b][:, lt, :], axis=AXIS.X, op=ALU.max, negate=True
             )
 
-        def prepare_weight(w_rows):
-            w_grouped = per_weight.tile([PART, CHANNELS * PACK], BF16, align_bytes=64)
-            w_codes = per_weight.tile([PART, CHANNELS], U32, align_bytes=64)
-            w_scales = per_weight.tile([PART, CHANNELS], U8, align_bytes=64)
-            transpose_words(w_rows, w_grouped, C_TILES, nc.scalar.copy)
-            quantise(w_grouped, w_codes, w_scales, 0, CHANNELS)
-            return w_codes, w_scales
-
-        def softmax_numerator(b):
-            neg_max = per_clip.tile([PART, L_TILES], F32)
-            e_sum = per_clip.tile([PART, L_TILES], F32)
-            e_rows = per_clip.tile([PART, L_TILES, PACK, PART], BF16)
-            for lt in range(L_TILES):
-                nc.vector.tensor_reduce(
-                    out=neg_max[:, lt : lt + 1], in_=att_rows[b][:, lt, :], axis=AXIS.X, op=ALU.max, negate=True
-                )
-                nc.scalar.activation(
-                    out=e_rows[:, lt, :, :].rearrange("l (u e) q -> l u e q", u=2),
-                    in_=att_rows[b][:, lt, :].rearrange("l (u q e) -> l u e q", u=2, e=2),
-                    func=ACT.Exp,
-                    bias=neg_max[:, lt : lt + 1],
-                    scale=1.0,
-                    accum_out=e_sum[:, lt : lt + 1],
-                )
-            return e_rows, e_sum
-
-        def prepare_g(b):
-            gm_grouped = per_clip.tile([PART, FEATURES * PACK], BF16, align_bytes=64)
-            gm_codes = per_clip.tile([PART, FEATURES], U32, align_bytes=64)
-            gm_scales = per_clip.tile([PART, FEATURES], U8, align_bytes=64)
-            transpose_words(g_rows[b], gm_grouped, P_TILES, nc.vector.tensor_copy)
-            gp_grouped = per_clip.tile([PART, POSITIONS * PACK], BF16, align_bytes=64)
-            gp_codes = per_clip.tile([PART, POSITIONS], U32, align_bytes=64)
-            gp_scales = per_clip.tile([PART, POSITIONS], U8, align_bytes=64)
-            nc.vector.tensor_copy(
-                out=gp_grouped[:].rearrange("q (c i t) -> q c t i", i=4, t=PACK),
-                in_=g_rows[b][:].rearrange("q (t c i) -> q c t i", t=PACK, i=4),
+        def exponential(b, lt):
+            nc.scalar.activation(
+                out=e_rows[b][:, lt, :, :].rearrange("l (u e) q -> l u e q", u=2),
+                in_=att_rows[b][:, lt, :].rearrange("l (u q e) -> l u e q", u=2, e=2),
+                func=ACT.Exp,
+                bias=neg_max[b][:, lt : lt + 1],
+                scale=1.0,
+                accum_out=e_sum[b][:, lt : lt + 1],
             )
-            quantise(gm_grouped, gm_codes, gm_scales, 0, FEATURES)
-            quantise(gp_grouped, gp_codes, gp_scales, 0, POSITIONS)
-            return gm_codes, gm_scales, gp_codes, gp_scales
 
-        def prepare_e(e_rows, e_sum):
-            e_grouped = per_clip.tile([PART, POSITIONS * PACK], BF16, align_bytes=64)
-            e_codes = per_clip.tile([PART, POSITIONS], U32, align_bytes=64)
-            e_scales = per_clip.tile([PART, POSITIONS], U8, align_bytes=64)
+        def transpose_e(b):
             for lt in range(L_TILES):
-                bank = psum_t.tile([PART, PACK, PART], BF16, tag="t")
+                acc = bank([PART, PACK, PART], BF16)
                 for t in range(PACK):
-                    nc.tensor.transpose(bank[:, t, :], e_rows[:, lt, t, :], ident_bf16[:])
+                    nc.tensor.transpose(acc[:, t, :], e_rows[b][:, lt, t, :], ident_bf16[:])
                 nc.scalar.copy(
-                    out=e_grouped[:, cols(lt, PACK * PART)].rearrange("q (l t) -> q l t", t=PACK),
-                    in_=bank[:].rearrange("q t l -> q l t"),
+                    out=e_by_m[b]["values"][:, cols(lt, PACK * PART)].rearrange("q (l t) -> q l t", t=PACK),
+                    in_=acc[:].rearrange("q t l -> q l t"),
                 )
-                quantise(e_grouped, e_codes, e_scales, lt, PART)
-            e_recip = per_clip.tile([PART, L_TILES], F32)
-            nc.vector.reciprocal(out=e_recip[:], in_=e_sum[:])
-            bank = psum_t.tile([PART, POSITIONS], F32, tag="t")
+
+        def spread_recip(b):
+            acc = bank([PART, POSITIONS], F32)
             for lt in range(L_TILES):
                 nc.tensor.transpose(
-                    bank[:, cols(lt, PART)], e_recip[:, lt : lt + 1].to_broadcast([PART, PART]), ident_f32[:]
+                    acc[:, cols(lt, PART)], e_recip[b][:, lt : lt + 1].to_broadcast([PART, PART]), ident_f32[:]
                 )
-            recip_rows = per_clip.tile([PART, POSITIONS], F32)
-            nc.scalar.copy(out=recip_rows[:], in_=bank[:])
-            return e_codes, e_scales, recip_rows
+            nc.scalar.copy(out=recip_rows[b][:], in_=acc[:])
 
-        def aggregate(e_codes, e_scales, gm_codes, gm_scales, recip_rows):
-            y_grouped = per_clip.tile([PART, POSITIONS * PACK], BF16, align_bytes=64)
-            y_codes = per_clip.tile([PART, POSITIONS], U32, align_bytes=64)
-            y_scales = per_clip.tile([PART, POSITIONS], U8, align_bytes=64)
-            for lt in range(L_TILES):
-                bank = psum_y.tile([PART, PACK, PART], F32)
-                for t in range(PACK):
-                    nc.tensor.matmul_mx(
-                        out=bank[:, t, :],
-                        lhsT=gm_codes[:, cols(t, PART)].bitcast(FP8X4),
-                        lhsT_scale=gm_scales[:, cols(t, PART)],
-                        rhs=e_codes[:, cols(lt, PART)].bitcast(FP8X4),
-                        rhs_scale=e_scales[:, cols(lt, PART)],
-                        start=True,
-                        stop=True,
-                    )
-                nc.vector.tensor_tensor(
-                    out=y_grouped[:, cols(lt, PACK * PART)].rearrange("q (l t) -> q l t", t=PACK),
-                    in0=bank[:].rearrange("q t l -> q l t"),
-                    in1=recip_rows[:, cols(lt, PART)].unsqueeze(2).to_broadcast([PART, PART, PACK]),
-                    op=ALU.mult,
-                )
-                quantise(y_grouped, y_codes, y_scales, lt, PART)
-            return y_codes, y_scales
+        def regroup_g(b):
+            nc.vector.tensor_copy(
+                out=g_by_p[b]["values"][:].rearrange("q (c i t) -> q c t i", i=4, t=PACK),
+                in_=g_rows[b][:].rearrange("q (t c i) -> q c t i", t=PACK, i=4),
+            )
 
-        def project(b, gp_codes, gp_scales, y_codes, y_scales):
-            result = per_clip.tile([PART, C_TILES, POSITIONS], F32)
-            out_rows = out[b].rearrange("(i ct) l -> i ct l", ct=C_TILES)
-            for ct in range(C_TILES):
-                bank = psum_o.tile([PART, POSITIONS], F32)
-                nc.tensor.matmul_mx(
-                    out=bank[:],
-                    lhsT=w1_codes[:, cols(ct, PART)].bitcast(FP8X4),
-                    lhsT_scale=w1_scales[:, cols(ct, PART)],
-                    rhs=gp_codes[:].bitcast(FP8X4),
-                    rhs_scale=gp_scales[:],
-                    start=True,
-                    stop=False,
-                )
-                nc.tensor.matmul_mx(
-                    out=bank[:],
-                    lhsT=w2_codes[:, cols(ct, PART)].bitcast(FP8X4),
-                    lhsT_scale=w2_scales[:, cols(ct, PART)],
-                    rhs=y_codes[:].bitcast(FP8X4),
-                    rhs_scale=y_scales[:],
-                    start=False,
-                    stop=True,
-                )
-                if ct % 3 == 2:
-                    nc.vector.tensor_scalar_add(out=result[:, ct, :], in0=bank[:], scalar1=bias[:, ct : ct + 1])
-                else:
-                    nc.scalar.activation(
-                        out=result[:, ct, :], in_=bank[:], func=ACT.Identity, bias=bias[:, ct : ct + 1], scale=1.0
-                    )
-                if ct % 2 == 1:
-                    nc.sync.dma_start(out=out_rows[:, ct - 1 : ct + 1, :], in_=result[:, ct - 1 : ct + 1, :])
+        def aggregate_multiply(b, lt):
+            acc = bank([PART, PACK, PART], F32)
+            for t in range(PACK):
+                multiply(acc[:, t, :], g_by_m[b], t, e_by_m[b], lt, PART, True, True)
+            return acc
 
-        e_rows_0, e_sum_0 = softmax_numerator(0)
-        gm_codes_0, gm_scales_0, gp_codes_0, gp_scales_0 = prepare_g(0)
-        e_codes_0, e_scales_0, recip_rows_0 = prepare_e(e_rows_0, e_sum_0)
-        w1_codes, w1_scales = prepare_weight(w1_rows)
-        y_codes_0, y_scales_0 = aggregate(e_codes_0, e_scales_0, gm_codes_0, gm_scales_0, recip_rows_0)
-        w2_codes, w2_scales = prepare_weight(w2_rows)
-        e_rows_1, e_sum_1 = softmax_numerator(1)
-        project(0, gp_codes_0, gp_scales_0, y_codes_0, y_scales_0)
-        gm_codes_1, gm_scales_1, gp_codes_1, gp_scales_1 = prepare_g(1)
-        e_codes_1, e_scales_1, recip_rows_1 = prepare_e(e_rows_1, e_sum_1)
-        y_codes_1, y_scales_1 = aggregate(e_codes_1, e_scales_1, gm_codes_1, gm_scales_1, recip_rows_1)
-        project(1, gp_codes_1, gp_scales_1, y_codes_1, y_scales_1)
+        def aggregate_divide(b, lt, acc):
+            nc.vector.tensor_tensor(
+                out=y_by_p[b]["values"][:, cols(lt, PACK * PART)].rearrange("q (l t) -> q l t", t=PACK),
+                in0=acc[:].rearrange("q t l -> q l t"),
+                in1=recip_rows[b][:, cols(lt, PART)].unsqueeze(2).to_broadcast([PART, PART, PACK]),
+                op=ALU.mult,
+            )
+            quantise(y_by_p[b], lt, PART)
+
+        def project_g(b, ct):
+            acc = bank([PART, POSITIONS], F32)
+            multiply(acc[:], w_by_p[0], ct, g_by_p[b], 0, POSITIONS, True, False)
+            return acc
+
+        def project_y(b, ct, acc, on_vector):
+            multiply(acc[:], w_by_p[1], ct, y_by_p[b], 0, POSITIONS, False, True)
+            if on_vector:
+                nc.vector.tensor_scalar_add(out=result[b][:, ct, :], in0=acc[:], scalar1=bias[:, ct : ct + 1])
+            else:
+                nc.scalar.activation(
+                    out=result[b][:, ct, :], in_=acc[:], func=ACT.Identity, bias=bias[:, ct : ct + 1], scale=1.0
+                )
+            if ct % 2 == 1:
+                out_rows = out[b].rearrange("(i ct) l -> i ct l", ct=C_TILES)
+                nc.sync.dma_start(out=out_rows[:, ct - 1 : ct + 1, :], in_=result[b][:, ct - 1 : ct + 1, :])
+
+        for lt in range(L_TILES):
+            row_max(0, lt)
+            exponential(0, lt)
+        transpose_words(g_rows[0], g_by_m[0], P_TILES, nc.vector.tensor_copy)
+        nc.vector.reciprocal(out=e_recip[0][:], in_=e_sum[0][:])
+        transpose_e(0)
+        spread_recip(0)
+        regroup_g(0)
+        quantise(g_by_m[0], 0, FEATURES)
+        quantise(g_by_p[0], 0, POSITIONS)
+        for lt in range(L_TILES):
+            quantise(e_by_m[0], lt, PART)
+
+        row_max(1, 0)
+        row_max(1, 1)
+        transpose_words(w_rows[0], w_by_p[0], C_TILES, nc.scalar.copy)
+        for lt in range(L_TILES):
+            aggregate_divide(0, lt, aggregate_multiply(0, lt))
+        transpose_words(w_rows[1], w_by_p[1], C_TILES, nc.scalar.copy)
+        row_max(1, 2)
+        row_max(1, 3)
+        for lt in range(L_TILES):
+            exponential(1, lt)
+        quantise(w_by_p[0], 0, CHANNELS)
+        quantise(w_by_p[1], 0, CHANNELS)
+        nc.vector.tensor_tensor(out=bias[:], in0=b1[:], in1=b2[:], op=ALU.add)
+
+        transpose_words(g_rows[1], g_by_m[1], P_TILES, nc.vector.tensor_copy)
+        nc.vector.reciprocal(out=e_recip[1][:], in_=e_sum[1][:])
+        transpose_e(1)
+        spread_recip(1)
+
+        for ct in range(C_TILES // 2):
+            project_y(0, ct, project_g(0, ct), False)
+        regroup_g(1)
+        quantise(g_by_m[1], 0, FEATURES)
+        quantise(g_by_p[1], 0, POSITIONS)
+        for lt in range(L_TILES):
+            quantise(e_by_m[1], lt, PART)
+        y_banks = [aggregate_multiply(1, lt) for lt in range(L_TILES)]
+        for ct in range(C_TILES // 2, C_TILES):
+            project_y(0, ct, project_g(0, ct), False)
+        for lt in range(L_TILES):
+            aggregate_divide(1, lt, y_banks[lt])
+
+        out_banks = [project_g(1, ct) for ct in range(C_TILES)]
+        for ct in range(C_TILES):
+            project_y(1, ct, out_banks[ct], ct % 2 == 1)

@@ -170,14 +170,17 @@ def tile_stnonlocalgnlstage_pb_kernel(tc, att_logits, g, w1_w, w1_b, w2_w, w2_b,
                 multiply(acc[:, t, :], g_by_m[b], t, e_by_m[b], lt, PART, True, True)
             return acc
 
-        def aggregate_divide(b, lt, acc):
-            nc.vector.tensor_tensor(
-                out=y_by_p[b]["values"][:, cols(lt, PACK * PART)].rearrange("q (l t) -> q l t", t=PACK),
-                in0=acc[:].rearrange("q t l -> q l t"),
-                in1=recip_rows[b][:, cols(lt, PART)].unsqueeze(2).to_broadcast([PART, PART, PACK]),
-                op=ALU.mult,
-            )
-            quantise(y_by_p[b], lt, PART)
+        def aggregate_divide(b, y_banks):
+            for lt in range(L_TILES):
+                nc.vector.tensor_tensor(
+                    out=y_by_p[b]["values"][:, cols(lt, PACK * PART)].rearrange("q (l t) -> q l t", t=PACK),
+                    in0=y_banks[lt][:].rearrange("q t l -> q l t"),
+                    in1=recip_rows[b][:, cols(lt, PART)].unsqueeze(2).to_broadcast([PART, PART, PACK]),
+                    op=ALU.mult,
+                )
+                if lt > 0:
+                    quantise(y_by_p[b], lt - 1, PART)
+            quantise(y_by_p[b], L_TILES - 1, PART)
 
         def project_g(b, ct):
             acc = bank([PART, POSITIONS], F32)
@@ -212,8 +215,7 @@ def tile_stnonlocalgnlstage_pb_kernel(tc, att_logits, g, w1_w, w1_b, w2_w, w2_b,
         row_max(1, 0)
         row_max(1, 1)
         transpose_words(w_rows[0], w_by_p[0], C_TILES, nc.scalar.copy)
-        for lt in range(L_TILES):
-            aggregate_divide(0, lt, aggregate_multiply(0, lt))
+        aggregate_divide(0, [aggregate_multiply(0, lt) for lt in range(L_TILES)])
         transpose_words(w_rows[1], w_by_p[1], C_TILES, nc.scalar.copy)
         row_max(1, 2)
         row_max(1, 3)
@@ -238,8 +240,7 @@ def tile_stnonlocalgnlstage_pb_kernel(tc, att_logits, g, w1_w, w1_b, w2_w, w2_b,
         y_banks = [aggregate_multiply(1, lt) for lt in range(L_TILES)]
         for ct in range(C_TILES // 2, C_TILES):
             project_y(0, ct, project_g(0, ct), False)
-        for lt in range(L_TILES):
-            aggregate_divide(1, lt, y_banks[lt])
+        aggregate_divide(1, y_banks)
 
         out_banks = [project_g(1, ct) for ct in range(C_TILES)]
         for ct in range(C_TILES):

@@ -68,8 +68,6 @@ def tile_stnonlocalgnlstage_pb_kernel(tc, att_logits, g, w1_w, w1_b, w2_w, w2_b,
 
         ident_f32 = sbuf.tile([PART, PART], F32)
         masks.make_identity(nc, ident_f32[:])
-        ident_bf16 = sbuf.tile([PART, PART], BF16)
-        masks.make_identity(nc, ident_bf16[:])
 
         warm = sbuf.tile([PART, 1], F32)
         nc.vector.memset(warm[:], 0.0)
@@ -84,7 +82,7 @@ def tile_stnonlocalgnlstage_pb_kernel(tc, att_logits, g, w1_w, w1_b, w2_w, w2_b,
         neg_max = [sbuf.tile([PART, L_TILES], F32, name="neg_max%d" % b) for b in range(CLIPS)]
         e_sum = [sbuf.tile([PART, L_TILES], F32, name="e_sum%d" % b) for b in range(CLIPS)]
         e_recip = [sbuf.tile([PART, L_TILES], F32, name="e_recip%d" % b) for b in range(CLIPS)]
-        e_rows = [sbuf.tile([PART, L_TILES, PACK, PART], BF16, name="e_rows%d" % b) for b in range(CLIPS)]
+        e_rows = [sbuf.tile([PART, L_TILES * POSITIONS], BF16, name="e_rows%d" % b) for b in range(CLIPS)]
         recip_rows = [sbuf.tile([PART, POSITIONS], F32, name="recip_rows%d" % b) for b in range(CLIPS)]
         result = [sbuf.tile([PART, C_TILES, POSITIONS], F32, name="result%d" % b) for b in range(CLIPS)]
         e_by_m = [mx_operand("e_by_m%d" % b, POSITIONS) for b in range(CLIPS)]
@@ -105,17 +103,17 @@ def tile_stnonlocalgnlstage_pb_kernel(tc, att_logits, g, w1_w, w1_b, w2_w, w2_b,
         for lt in range(L_TILES):
             nc.sync.dma_start(out=att_rows[0][:, lt, :], in_=att_logits[0, cols(lt, PART), :])
         load_g(0)
+        nc.sync.dma_start(out=att_rows[1][:], in_=att_logits[1].rearrange("(lt l) m -> l lt m", l=PART))
         load_w(0, w1_w)
         load_w(1, w2_w)
-        nc.sync.dma_start(out=att_rows[1][:], in_=att_logits[1].rearrange("(lt l) m -> l lt m", l=PART))
         load_g(1)
         nc.sync.dma_start(out=b1[:], in_=w1_b.rearrange("(i ct) -> i ct", ct=C_TILES))
         nc.sync.dma_start(out=b2[:], in_=w2_b.rearrange("(i ct) -> i ct", ct=C_TILES))
 
-        def transpose_words(rows, operand, n_blocks, copy):
+        def transpose_words(rows, operand, pairs, copy):
             words = rows[:].bitcast(F32)
             value_words = operand["values"][:].bitcast(F32)
-            for pair in range(n_blocks // 2):
+            for pair in pairs:
                 acc = bank([PART, 2, 2, PART], F32)
                 for n in range(2):
                     for u in range(2):
@@ -132,23 +130,13 @@ def tile_stnonlocalgnlstage_pb_kernel(tc, att_logits, g, w1_w, w1_b, w2_w, w2_b,
 
         def exponential(b, lt):
             nc.scalar.activation(
-                out=e_rows[b][:, lt, :, :].rearrange("l (u e) q -> l u e q", u=2),
-                in_=att_rows[b][:, lt, :].rearrange("l (u q e) -> l u e q", u=2, e=2),
+                out=e_rows[b][:, cols(lt, POSITIONS)],
+                in_=att_rows[b][:, lt, :],
                 func=ACT.Exp,
                 bias=neg_max[b][:, lt : lt + 1],
                 scale=1.0,
                 accum_out=e_sum[b][:, lt : lt + 1],
             )
-
-        def transpose_e(b):
-            for lt in range(L_TILES):
-                acc = bank([PART, PACK, PART], BF16)
-                for t in range(PACK):
-                    nc.tensor.transpose(acc[:, t, :], e_rows[b][:, lt, t, :], ident_bf16[:])
-                nc.scalar.copy(
-                    out=e_by_m[b]["values"][:, cols(lt, PACK * PART)].rearrange("q (l t) -> q l t", t=PACK),
-                    in_=acc[:].rearrange("q t l -> q l t"),
-                )
 
         def spread_recip(b):
             acc = bank([PART, POSITIONS], F32)
@@ -187,8 +175,10 @@ def tile_stnonlocalgnlstage_pb_kernel(tc, att_logits, g, w1_w, w1_b, w2_w, w2_b,
             multiply(acc[:], w_by_p[0], ct, g_by_p[b], 0, POSITIONS, True, False)
             return acc
 
-        def project_y(b, ct, acc, on_vector):
+        def project_y(b, ct, acc):
             multiply(acc[:], w_by_p[1], ct, y_by_p[b], 0, POSITIONS, False, True)
+
+        def leave(b, ct, acc, on_vector):
             if on_vector:
                 nc.vector.tensor_scalar_add(out=result[b][:, ct, :], in0=acc[:], scalar1=bias[:, ct : ct + 1])
             else:
@@ -199,49 +189,61 @@ def tile_stnonlocalgnlstage_pb_kernel(tc, att_logits, g, w1_w, w1_b, w2_w, w2_b,
                 out_rows = out[b].rearrange("(i ct) l -> i ct l", ct=C_TILES)
                 nc.sync.dma_start(out=out_rows[:, ct - 1 : ct + 1, :], in_=result[b][:, ct - 1 : ct + 1, :])
 
+        def project(b, ct, on_vector):
+            acc = project_g(b, ct)
+            project_y(b, ct, acc)
+            leave(b, ct, acc, on_vector)
+
         for lt in range(L_TILES):
             row_max(0, lt)
             exponential(0, lt)
-        transpose_words(g_rows[0], g_by_m[0], P_TILES, nc.vector.tensor_copy)
-        nc.vector.reciprocal(out=e_recip[0][:], in_=e_sum[0][:])
-        transpose_e(0)
-        spread_recip(0)
+        transpose_words(g_rows[0], g_by_m[0], range(P_TILES // 2), nc.scalar.copy)
         regroup_g(0)
-        quantise(g_by_m[0], 0, FEATURES)
-        quantise(g_by_p[0], 0, POSITIONS)
-        for lt in range(L_TILES):
-            quantise(e_by_m[0], lt, PART)
-
         row_max(1, 0)
         row_max(1, 1)
-        transpose_words(w_rows[0], w_by_p[0], C_TILES, nc.scalar.copy)
-        aggregate_divide(0, [aggregate_multiply(0, lt) for lt in range(L_TILES)])
-        transpose_words(w_rows[1], w_by_p[1], C_TILES, nc.scalar.copy)
+        nc.vector.reciprocal(out=e_recip[0][:], in_=e_sum[0][:])
+        transpose_words(e_rows[0], e_by_m[0], range(L_TILES // 2), nc.scalar.copy)
+        spread_recip(0)
+        quantise(g_by_p[0], 0, POSITIONS)
+        quantise(g_by_m[0], 0, FEATURES)
+        for pair in range(L_TILES // 2):
+            quantise(e_by_m[0], pair, 2 * PART)
         row_max(1, 2)
         row_max(1, 3)
+
+        transpose_words(w_rows[0], w_by_p[0], range(C_TILES // 2), nc.scalar.copy)
+        aggregate_divide(0, [aggregate_multiply(0, lt) for lt in range(L_TILES)])
+        transpose_words(w_rows[1], w_by_p[1], range(C_TILES // 2), nc.scalar.copy)
         for lt in range(L_TILES):
             exponential(1, lt)
         quantise(w_by_p[0], 0, CHANNELS)
         quantise(w_by_p[1], 0, CHANNELS)
         nc.vector.tensor_tensor(out=bias[:], in0=b1[:], in1=b2[:], op=ALU.add)
 
-        transpose_words(g_rows[1], g_by_m[1], P_TILES, nc.vector.tensor_copy)
+        transpose_words(g_rows[1], g_by_m[1], range(P_TILES // 2), nc.vector.tensor_copy)
+        transpose_words(e_rows[1], e_by_m[1], [0], nc.scalar.copy)
+        first_banks = [project_g(0, ct) for ct in range(2)]
+        for ct in range(2):
+            project_y(0, ct, first_banks[ct])
         nc.vector.reciprocal(out=e_recip[1][:], in_=e_sum[1][:])
-        transpose_e(1)
+        transpose_words(e_rows[1], e_by_m[1], [1], nc.scalar.copy)
         spread_recip(1)
-
-        for ct in range(C_TILES // 2):
-            project_y(0, ct, project_g(0, ct), False)
-        regroup_g(1)
         quantise(g_by_m[1], 0, FEATURES)
+        quantise(e_by_m[1], 0, 2 * PART)
+        regroup_g(1)
+        quantise(e_by_m[1], 1, 2 * PART)
         quantise(g_by_p[1], 0, POSITIONS)
-        for lt in range(L_TILES):
-            quantise(e_by_m[1], lt, PART)
+        for ct in range(2):
+            leave(0, ct, first_banks[ct], False)
+
+        for ct in range(2, C_TILES // 2):
+            project(0, ct, False)
         y_banks = [aggregate_multiply(1, lt) for lt in range(L_TILES)]
         for ct in range(C_TILES // 2, C_TILES):
-            project_y(0, ct, project_g(0, ct), False)
+            project(0, ct, False)
         aggregate_divide(1, y_banks)
 
         out_banks = [project_g(1, ct) for ct in range(C_TILES)]
         for ct in range(C_TILES):
-            project_y(1, ct, out_banks[ct], ct % 2 == 1)
+            project_y(1, ct, out_banks[ct])
+            leave(1, ct, out_banks[ct], ct % 2 == 1)

@@ -22,6 +22,7 @@ PACK = 4
 L_TILES = POSITIONS // PART
 P_TILES = FEATURES // PART
 C_TILES = CHANNELS // PART
+HALF = POSITIONS // 2
 PSUM_BANKS = 8
 
 FLOPS = 2 * CLIPS * (POSITIONS * POSITIONS * FEATURES + 2 * POSITIONS * FEATURES * CHANNELS)
@@ -170,29 +171,38 @@ def tile_stnonlocalgnlstage_pb_kernel(tc, att_logits, g, w1_w, w1_b, w2_w, w2_b,
                     quantise(y_by_p[b], lt - 1, PART)
             quantise(y_by_p[b], L_TILES - 1, PART)
 
-        def project_g(b, ct):
-            acc = bank([PART, POSITIONS], F32)
-            multiply(acc[:], w_by_p[0], ct, g_by_p[b], 0, POSITIONS, True, False)
+        def project_g(b, ct, piece, width):
+            acc = bank([PART, width], F32)
+            multiply(acc[:], w_by_p[0], ct, g_by_p[b], piece, width, True, False)
             return acc
 
-        def project_y(b, ct, acc):
-            multiply(acc[:], w_by_p[1], ct, y_by_p[b], 0, POSITIONS, False, True)
+        def project_y(b, ct, piece, width, acc):
+            multiply(acc[:], w_by_p[1], ct, y_by_p[b], piece, width, False, True)
 
-        def leave(b, ct, acc, on_vector):
+        def leave(b, ct, piece, width, acc, on_vector):
             if on_vector:
-                nc.vector.tensor_scalar_add(out=result[b][:, ct, :], in0=acc[:], scalar1=bias[:, ct : ct + 1])
+                nc.vector.tensor_scalar_add(
+                    out=result[b][:, ct, cols(piece, width)], in0=acc[:], scalar1=bias[:, ct : ct + 1]
+                )
             else:
                 nc.scalar.activation(
-                    out=result[b][:, ct, :], in_=acc[:], func=ACT.Identity, bias=bias[:, ct : ct + 1], scale=1.0
+                    out=result[b][:, ct, cols(piece, width)],
+                    in_=acc[:],
+                    func=ACT.Identity,
+                    bias=bias[:, ct : ct + 1],
+                    scale=1.0,
                 )
             if ct % 2 == 1:
                 out_rows = out[b].rearrange("(i ct) l -> i ct l", ct=C_TILES)
-                nc.sync.dma_start(out=out_rows[:, ct - 1 : ct + 1, :], in_=result[b][:, ct - 1 : ct + 1, :])
+                nc.sync.dma_start(
+                    out=out_rows[:, ct - 1 : ct + 1, cols(piece, width)],
+                    in_=result[b][:, ct - 1 : ct + 1, cols(piece, width)],
+                )
 
-        def project(b, ct, on_vector):
-            acc = project_g(b, ct)
-            project_y(b, ct, acc)
-            leave(b, ct, acc, on_vector)
+        def project(b, ct, piece, width, on_vector):
+            acc = project_g(b, ct, piece, width)
+            project_y(b, ct, piece, width, acc)
+            leave(b, ct, piece, width, acc, on_vector)
 
         for lt in range(L_TILES):
             row_max(0, lt)
@@ -222,9 +232,9 @@ def tile_stnonlocalgnlstage_pb_kernel(tc, att_logits, g, w1_w, w1_b, w2_w, w2_b,
 
         transpose_words(g_rows[1], g_by_m[1], range(P_TILES // 2), nc.vector.tensor_copy)
         transpose_words(e_rows[1], e_by_m[1], [0], nc.scalar.copy)
-        first_banks = [project_g(0, ct) for ct in range(2)]
+        first_banks = [project_g(0, ct, 0, POSITIONS) for ct in range(2)]
         for ct in range(2):
-            project_y(0, ct, first_banks[ct])
+            project_y(0, ct, 0, POSITIONS, first_banks[ct])
         nc.vector.reciprocal(out=e_recip[1][:], in_=e_sum[1][:])
         transpose_words(e_rows[1], e_by_m[1], [1], nc.scalar.copy)
         spread_recip(1)
@@ -234,16 +244,18 @@ def tile_stnonlocalgnlstage_pb_kernel(tc, att_logits, g, w1_w, w1_b, w2_w, w2_b,
         quantise(e_by_m[1], 1, 2 * PART)
         quantise(g_by_p[1], 0, POSITIONS)
         for ct in range(2):
-            leave(0, ct, first_banks[ct], False)
+            leave(0, ct, 0, POSITIONS, first_banks[ct], False)
 
         for ct in range(2, C_TILES // 2):
-            project(0, ct, False)
+            project(0, ct, 0, POSITIONS, False)
         y_banks = [aggregate_multiply(1, lt) for lt in range(L_TILES)]
         for ct in range(C_TILES // 2, C_TILES):
-            project(0, ct, False)
+            project(0, ct, 0, POSITIONS, False)
         aggregate_divide(1, y_banks)
 
-        out_banks = [project_g(1, ct) for ct in range(C_TILES)]
+        half_banks = [project_g(1, ct, 0, HALF) for ct in range(C_TILES)]
         for ct in range(C_TILES):
-            project_y(1, ct, out_banks[ct])
-            leave(1, ct, out_banks[ct], ct % 2 == 1)
+            project_y(1, ct, 0, HALF, half_banks[ct])
+            leave(1, ct, 0, HALF, half_banks[ct], ct % 2 == 1)
+        for ct in range(C_TILES):
+            project(1, ct, 1, HALF, ct % 2 == 1)

@@ -111,7 +111,7 @@ def tile_stnonlocalgnlstage_pb_kernel(tc, att_logits, g, w1_w, w1_b, w2_w, w2_b,
         nc.sync.dma_start(out=b1[:], in_=w1_b.rearrange("(i ct) -> i ct", ct=C_TILES))
         nc.sync.dma_start(out=b2[:], in_=w2_b.rearrange("(i ct) -> i ct", ct=C_TILES))
 
-        def transpose_words(rows, operand, pairs, copy):
+        def transpose_words(rows, operand, pairs, copy, busy_width=0):
             words = rows[:].bitcast(F32)
             value_words = operand["values"][:].bitcast(F32)
             for pair in pairs:
@@ -119,6 +119,8 @@ def tile_stnonlocalgnlstage_pb_kernel(tc, att_logits, g, w1_w, w1_b, w2_w, w2_b,
                 for n in range(2):
                     for u in range(2):
                         nc.tensor.transpose(acc[:, n, u, :], words[:, cols(4 * pair + 2 * n + u, PART)], ident_f32[:])
+                if busy_width:
+                    keep_busy(1, busy_width)
                 copy(
                     out=value_words[:, cols(pair, 4 * PART)].rearrange("q (n r u) -> q n r u", n=2, u=2),
                     in_=acc[:].rearrange("q n u r -> q n r u"),
@@ -199,20 +201,29 @@ def tile_stnonlocalgnlstage_pb_kernel(tc, att_logits, g, w1_w, w1_b, w2_w, w2_b,
                     in_=result[b][:, ct - 1 : ct + 1, cols(piece, width)],
                 )
 
+        def keep_busy(times, width):
+            acc = bank([PART, POSITIONS], F32)
+            for i in range(times):
+                nc.tensor.matmul(
+                    acc[:, :width], lhsT=att_rows[0][:, 0, :PART], rhs=att_rows[0][:, 0, :width], start=True, stop=True
+                )
+
         def project(b, ct, piece, width, on_vector):
             acc = project_g(b, ct, piece, width)
             project_y(b, ct, piece, width, acc)
             leave(b, ct, piece, width, acc, on_vector)
 
+        keep_busy(4, POSITIONS)
+
         for lt in range(L_TILES):
             row_max(0, lt)
             exponential(0, lt)
-        transpose_words(g_rows[0], g_by_m[0], range(P_TILES // 2), nc.scalar.copy)
+        transpose_words(g_rows[0], g_by_m[0], range(P_TILES // 2), nc.scalar.copy, HALF)
         regroup_g(0)
         row_max(1, 0)
         row_max(1, 1)
         nc.vector.reciprocal(out=e_recip[0][:], in_=e_sum[0][:])
-        transpose_words(e_rows[0], e_by_m[0], range(L_TILES // 2), nc.scalar.copy)
+        transpose_words(e_rows[0], e_by_m[0], range(L_TILES // 2), nc.scalar.copy, POSITIONS)
         spread_recip(0)
         quantise(g_by_p[0], 0, POSITIONS)
         quantise(g_by_m[0], 0, FEATURES)
@@ -221,16 +232,16 @@ def tile_stnonlocalgnlstage_pb_kernel(tc, att_logits, g, w1_w, w1_b, w2_w, w2_b,
         row_max(1, 2)
         row_max(1, 3)
 
-        transpose_words(w_rows[0], w_by_p[0], range(C_TILES // 2), nc.scalar.copy)
+        transpose_words(w_rows[0], w_by_p[0], range(C_TILES // 2), nc.scalar.copy, HALF)
         aggregate_divide(0, [aggregate_multiply(0, lt) for lt in range(L_TILES)])
-        transpose_words(w_rows[1], w_by_p[1], range(C_TILES // 2), nc.scalar.copy)
+        transpose_words(w_rows[1], w_by_p[1], range(C_TILES // 2), nc.scalar.copy, HALF)
         for lt in range(L_TILES):
             exponential(1, lt)
         quantise(w_by_p[0], 0, CHANNELS)
         quantise(w_by_p[1], 0, CHANNELS)
         nc.vector.tensor_tensor(out=bias[:], in0=b1[:], in1=b2[:], op=ALU.add)
 
-        transpose_words(g_rows[1], g_by_m[1], range(P_TILES // 2), nc.vector.tensor_copy)
+        transpose_words(g_rows[1], g_by_m[1], range(P_TILES // 2), nc.vector.tensor_copy, HALF)
         transpose_words(e_rows[1], e_by_m[1], [0], nc.scalar.copy)
         first_banks = [project_g(0, ct, 0, POSITIONS) for ct in range(2)]
         for ct in range(2):

@@ -23,7 +23,13 @@ L_TILES = POSITIONS // PART
 P_TILES = FEATURES // PART
 C_TILES = CHANNELS // PART
 HALF = POSITIONS // 2
-PSUM_BANKS = 8
+BANKS = {
+    "turned": (0, 1, 2, 3),
+    "y": (4, 5, 6),
+    "unread": (7,),
+    "out0": (7, 0, 1, 2),
+    "out1": (3, 5, 6, 7, 0, 4, 1, 2),
+}
 
 FLOPS = 2 * CLIPS * (POSITIONS * POSITIONS * FEATURES + 2 * POSITIONS * FEATURES * CHANNELS)
 
@@ -36,11 +42,15 @@ def tile_stnonlocalgnlstage_pb_kernel(tc, att_logits, g, w1_w, w1_b, w2_w, w2_b,
     nc = tc.nc
     with ExitStack() as ctx:
         sbuf = ctx.enter_context(tc.tile_pool(name="sbuf", bufs=1))
-        psum = ctx.enter_context(tc.psum_pool(name="psum", bufs=PSUM_BANKS))
+        psum = ctx.enter_context(tc.psum_pool(name="psum", bufs=1))
         ctx.enter_context(tc.manual_schedule())
 
-        def bank(shape, dtype):
-            return psum.tile(shape, dtype, name="bank", tag="bank")
+        turns = {}
+
+        def bank(shape, dtype, use):
+            turns[use] = turns.get(use, -1) + 1
+            tag = "bank%d" % BANKS[use][turns[use] % len(BANKS[use])]
+            return psum.tile(shape, dtype, name=tag, tag=tag)
 
         def mx_operand(name, n_cols):
             return {
@@ -98,33 +108,46 @@ def tile_stnonlocalgnlstage_pb_kernel(tc, att_logits, g, w1_w, w1_b, w2_w, w2_b,
                 in_=g[b].rearrange("(u j e) m -> j u e m", u=2, e=2),
             )
 
-        def load_w(i, w):
-            nc.sync.dma_start(out=w_rows[i][:], in_=w.rearrange("(i ct) p -> i (ct p)", ct=C_TILES))
+        def load_w(i, w, half):
+            nc.sync.dma_start(
+                out=w_rows[i][:, cols(half, C_TILES * FEATURES // 2)],
+                in_=w.rearrange("(i ct) p -> i (ct p)", ct=C_TILES)[:, cols(half, C_TILES * FEATURES // 2)],
+            )
+
+        def load_att(b, half):
+            nc.sync.dma_start(
+                out=att_rows[b][:, cols(half, L_TILES // 2), :],
+                in_=att_logits[b, cols(half, HALF), :].rearrange("(lt l) m -> l lt m", l=PART),
+            )
 
         for lt in range(L_TILES):
             nc.sync.dma_start(out=att_rows[0][:, lt, :], in_=att_logits[0, cols(lt, PART), :])
         load_g(0)
-        nc.sync.dma_start(out=att_rows[1][:], in_=att_logits[1].rearrange("(lt l) m -> l lt m", l=PART))
-        load_w(0, w1_w)
-        load_w(1, w2_w)
+        for half in range(2):
+            load_att(1, half)
+        for i, w in enumerate((w1_w, w2_w)):
+            for half in range(2):
+                load_w(i, w, half)
         load_g(1)
         nc.sync.dma_start(out=b1[:], in_=w1_b.rearrange("(i ct) -> i ct", ct=C_TILES))
         nc.sync.dma_start(out=b2[:], in_=w2_b.rearrange("(i ct) -> i ct", ct=C_TILES))
 
-        def transpose_words(rows, operand, pairs, copy, busy_width=0):
+        def transpose_words(rows, pair, use="turned"):
             words = rows[:].bitcast(F32)
-            value_words = operand["values"][:].bitcast(F32)
-            for pair in pairs:
-                acc = bank([PART, 2, 2, PART], F32)
-                for n in range(2):
-                    for u in range(2):
-                        nc.tensor.transpose(acc[:, n, u, :], words[:, cols(4 * pair + 2 * n + u, PART)], ident_f32[:])
-                if busy_width:
-                    keep_busy(1, busy_width)
-                copy(
-                    out=value_words[:, cols(pair, 4 * PART)].rearrange("q (n r u) -> q n r u", n=2, u=2),
-                    in_=acc[:].rearrange("q n u r -> q n r u"),
-                )
+            acc = bank([PART, 2, 2, PART], F32, use)
+            for n in range(2):
+                for u in range(2):
+                    nc.tensor.transpose(acc[:, n, u, :], words[:, cols(4 * pair + 2 * n + u, PART)], ident_f32[:])
+            return acc
+
+        def copy_words(acc, operand, pair, copy):
+            copy(
+                out=operand["values"][:].bitcast(F32)[:, cols(pair, 4 * PART)].rearrange("q (n r u) -> q n r u", n=2, u=2),
+                in_=acc[:].rearrange("q n u r -> q n r u"),
+            )
+
+        def turn(rows, operand, pair, copy):
+            copy_words(transpose_words(rows, pair), operand, pair, copy)
 
         def row_max(b, lt):
             nc.vector.tensor_reduce(
@@ -142,12 +165,12 @@ def tile_stnonlocalgnlstage_pb_kernel(tc, att_logits, g, w1_w, w1_b, w2_w, w2_b,
             )
 
         def spread_recip(b):
-            acc = bank([PART, POSITIONS], F32)
+            acc = bank([PART, POSITIONS], F32, "turned")
             for lt in range(L_TILES):
                 nc.tensor.transpose(
                     acc[:, cols(lt, PART)], e_recip[b][:, lt : lt + 1].to_broadcast([PART, PART]), ident_f32[:]
                 )
-            nc.scalar.copy(out=recip_rows[b][:], in_=acc[:])
+            return acc
 
         def regroup_g(b):
             nc.vector.tensor_copy(
@@ -156,25 +179,21 @@ def tile_stnonlocalgnlstage_pb_kernel(tc, att_logits, g, w1_w, w1_b, w2_w, w2_b,
             )
 
         def aggregate_multiply(b, lt):
-            acc = bank([PART, PACK, PART], F32)
+            acc = bank([PART, PACK, PART], F32, "y")
             for t in range(PACK):
                 multiply(acc[:, t, :], g_by_m[b], t, e_by_m[b], lt, PART, True, True)
             return acc
 
-        def aggregate_divide(b, y_banks):
-            for lt in range(L_TILES):
-                nc.vector.tensor_tensor(
-                    out=y_by_p[b]["values"][:, cols(lt, PACK * PART)].rearrange("q (l t) -> q l t", t=PACK),
-                    in0=y_banks[lt][:].rearrange("q t l -> q l t"),
-                    in1=recip_rows[b][:, cols(lt, PART)].unsqueeze(2).to_broadcast([PART, PART, PACK]),
-                    op=ALU.mult,
-                )
-                if lt > 0:
-                    quantise(y_by_p[b], lt - 1, PART)
-            quantise(y_by_p[b], L_TILES - 1, PART)
+        def aggregate_divide(b, lt, acc):
+            nc.vector.tensor_tensor(
+                out=y_by_p[b]["values"][:, cols(lt, PACK * PART)].rearrange("q (l t) -> q l t", t=PACK),
+                in0=acc[:].rearrange("q t l -> q l t"),
+                in1=recip_rows[b][:, cols(lt, PART)].unsqueeze(2).to_broadcast([PART, PART, PACK]),
+                op=ALU.mult,
+            )
 
         def project_g(b, ct, piece, width):
-            acc = bank([PART, width], F32)
+            acc = bank([PART, width], F32, "out%d" % b)
             multiply(acc[:], w_by_p[0], ct, g_by_p[b], piece, width, True, False)
             return acc
 
@@ -202,7 +221,7 @@ def tile_stnonlocalgnlstage_pb_kernel(tc, att_logits, g, w1_w, w1_b, w2_w, w2_b,
                 )
 
         def keep_busy(times, width):
-            acc = bank([PART, POSITIONS], F32)
+            acc = bank([PART, POSITIONS], F32, "unread")
             for i in range(times):
                 nc.tensor.matmul(
                     acc[:, :width], lhsT=att_rows[0][:, 0, :PART], rhs=att_rows[0][:, 0, :width], start=True, stop=True
@@ -213,60 +232,104 @@ def tile_stnonlocalgnlstage_pb_kernel(tc, att_logits, g, w1_w, w1_b, w2_w, w2_b,
             project_y(b, ct, piece, width, acc)
             leave(b, ct, piece, width, acc, on_vector)
 
+        vector_copy, scalar_copy = nc.vector.tensor_copy, nc.scalar.copy
+        half_channels = CHANNELS // 2
+
         keep_busy(4, POSITIONS)
 
         for lt in range(L_TILES):
             row_max(0, lt)
             exponential(0, lt)
-        transpose_words(g_rows[0], g_by_m[0], range(P_TILES // 2), nc.scalar.copy, HALF)
+        for pair in range(2):
+            turn(g_rows[0], g_by_m[0], pair, scalar_copy)
+            keep_busy(1, HALF)
         regroup_g(0)
         row_max(1, 0)
         row_max(1, 1)
+        for pair in range(2):
+            turn(e_rows[0], e_by_m[0], pair, scalar_copy)
+            keep_busy(1, POSITIONS)
         nc.vector.reciprocal(out=e_recip[0][:], in_=e_sum[0][:])
-        transpose_words(e_rows[0], e_by_m[0], range(L_TILES // 2), nc.scalar.copy, POSITIONS)
-        spread_recip(0)
+        nc.scalar.copy(out=recip_rows[0][:], in_=spread_recip(0)[:])
         quantise(g_by_p[0], 0, POSITIONS)
         quantise(g_by_m[0], 0, FEATURES)
-        for pair in range(L_TILES // 2):
+        for pair in range(2):
             quantise(e_by_m[0], pair, 2 * PART)
         row_max(1, 2)
+
+        for pair in range(2):
+            turn(w_rows[0], w_by_p[0], pair, scalar_copy)
+            keep_busy(1, HALF)
+        y_banks = [aggregate_multiply(0, lt) for lt in range(2)]
+        exponential(1, 0)
+        exponential(1, 1)
+        aggregate_divide(0, 0, y_banks[0])
         row_max(1, 3)
+        for pair in range(2, 4):
+            turn(w_rows[0], w_by_p[0], pair, scalar_copy)
+            keep_busy(1, HALF)
+        y_banks += [aggregate_multiply(0, lt) for lt in range(2, 4)]
+        exponential(1, 2)
+        exponential(1, 3)
+        for lt in range(1, L_TILES):
+            aggregate_divide(0, lt, y_banks[lt])
+            quantise(y_by_p[0], lt - 1, PART)
 
-        transpose_words(w_rows[0], w_by_p[0], range(C_TILES // 2), nc.scalar.copy, HALF)
-        aggregate_divide(0, [aggregate_multiply(0, lt) for lt in range(L_TILES)])
-        transpose_words(w_rows[1], w_by_p[1], range(C_TILES // 2), nc.scalar.copy, HALF)
-        for lt in range(L_TILES):
-            exponential(1, lt)
-        quantise(w_by_p[0], 0, CHANNELS)
-        quantise(w_by_p[1], 0, CHANNELS)
+        for pair in range(2):
+            turn(w_rows[1], w_by_p[1], pair, scalar_copy)
+            keep_busy(1, HALF)
+        quantise(w_by_p[0], 0, half_channels)
+        quantise(y_by_p[0], L_TILES - 1, PART)
+        quantise(w_by_p[0], 1, half_channels)
+        e_banks = [transpose_words(e_rows[1], 0, "y")]
+        nc.vector.reciprocal(out=e_recip[1][:], in_=e_sum[1][:])
+        for pair in range(2, 4):
+            turn(w_rows[1], w_by_p[1], pair, scalar_copy)
+            keep_busy(1, HALF)
+        quantise(w_by_p[1], 0, half_channels)
+        e_banks += [transpose_words(e_rows[1], 1, "y")]
+        turn(g_rows[1], g_by_m[1], 0, scalar_copy)
+        turn(g_rows[1], g_by_m[1], 1, vector_copy)
+        copy_words(e_banks[0], e_by_m[1], 0, scalar_copy)
+        quantise(w_by_p[1], 1, half_channels)
         nc.vector.tensor_tensor(out=bias[:], in0=b1[:], in1=b2[:], op=ALU.add)
+        recip_bank = spread_recip(1)
 
-        transpose_words(g_rows[1], g_by_m[1], range(P_TILES // 2), nc.vector.tensor_copy, HALF)
-        transpose_words(e_rows[1], e_by_m[1], [0], nc.scalar.copy)
         first_banks = [project_g(0, ct, 0, POSITIONS) for ct in range(2)]
         for ct in range(2):
             project_y(0, ct, 0, POSITIONS, first_banks[ct])
-        nc.vector.reciprocal(out=e_recip[1][:], in_=e_sum[1][:])
-        transpose_words(e_rows[1], e_by_m[1], [1], nc.scalar.copy)
-        spread_recip(1)
-        quantise(g_by_m[1], 0, FEATURES)
-        quantise(e_by_m[1], 0, 2 * PART)
-        regroup_g(1)
-        quantise(e_by_m[1], 1, 2 * PART)
-        quantise(g_by_p[1], 0, POSITIONS)
         for ct in range(2):
             leave(0, ct, 0, POSITIONS, first_banks[ct], False)
-
-        for ct in range(2, C_TILES // 2):
+        quantise(g_by_m[1], 0, FEATURES)
+        quantise(e_by_m[1], 0, 2 * PART)
+        copy_words(e_banks[1], e_by_m[1], 1, scalar_copy)
+        nc.scalar.copy(out=recip_rows[1][:], in_=recip_bank[:])
+        regroup_g(1)
+        quantise(e_by_m[1], 1, 2 * PART)
+        for ct in range(2, 4):
             project(0, ct, 0, POSITIONS, False)
-        y_banks = [aggregate_multiply(1, lt) for lt in range(L_TILES)]
-        for ct in range(C_TILES // 2, C_TILES):
+        y_banks = [aggregate_multiply(1, lt) for lt in range(2)]
+        for lt in range(2):
+            aggregate_divide(1, lt, y_banks[lt])
+        quantise(g_by_p[1], 0, POSITIONS)
+        quantise(y_by_p[1], 0, PART)
+        for ct in range(4, 6):
             project(0, ct, 0, POSITIONS, False)
-        aggregate_divide(1, y_banks)
+        y_banks += [aggregate_multiply(1, lt) for lt in range(2, 4)]
+        for ct in range(6, 8):
+            project(0, ct, 0, POSITIONS, False)
+        for lt in range(2, L_TILES):
+            aggregate_divide(1, lt, y_banks[lt])
+            quantise(y_by_p[1], lt - 1, PART)
+        quantise(y_by_p[1], L_TILES - 1, PART)
 
-        half_banks = [project_g(1, ct, 0, HALF) for ct in range(C_TILES)]
-        for ct in range(C_TILES):
-            project_y(1, ct, 0, HALF, half_banks[ct])
-            leave(1, ct, 0, HALF, half_banks[ct], ct % 2 == 1)
-        for ct in range(C_TILES):
-            project(1, ct, 1, HALF, ct % 2 == 1)
+        tiles = [(piece, ct) for piece in range(2) for ct in range(C_TILES)]
+        banks = []
+        for i in range(len(tiles) + 4):
+            if i < len(tiles):
+                piece, ct = tiles[i]
+                banks.append(project_g(1, ct, piece, HALF))
+            if i >= 4:
+                piece, ct = tiles[i - 4]
+                project_y(1, ct, piece, HALF, banks[i - 4])
+                leave(1, ct, piece, HALF, banks[i - 4], ct % 2 == 1)

@@ -25,10 +25,12 @@ C_TILES = CHANNELS // PART
 HALF = POSITIONS // 2
 BANKS = {
     "turned": (0, 1, 2, 3),
-    "y": (4, 5, 6),
+    "y0": (4, 5, 6),
+    "e1": (5, 6),
     "unread": (7,),
-    "out0": (7, 0, 1, 2),
-    "out1": (3, 5, 6, 7, 0, 4, 1, 2),
+    "out0": (7, 4, 0, 1),
+    "y1": (5, 2, 6, 3),
+    "out1": (5, 2, 7, 4, 6, 0, 3, 1),
 }
 
 FLOPS = 2 * CLIPS * (POSITIONS * POSITIONS * FEATURES + 2 * POSITIONS * FEATURES * CHANNELS)
@@ -90,6 +92,8 @@ def tile_stnonlocalgnlstage_pb_kernel(tc, att_logits, g, w1_w, w1_b, w2_w, w2_b,
         b1 = sbuf.tile([PART, C_TILES], BF16)
         b2 = sbuf.tile([PART, C_TILES], BF16)
         bias = sbuf.tile([PART, C_TILES], F32)
+        fold_2 = sbuf.tile([PART, L_TILES, HALF], BF16)
+        fold_4 = sbuf.tile([PART, L_TILES, PART], BF16)
         neg_max = [sbuf.tile([PART, L_TILES], F32, name="neg_max%d" % b) for b in range(CLIPS)]
         e_sum = [sbuf.tile([PART, L_TILES], F32, name="e_sum%d" % b) for b in range(CLIPS)]
         e_recip = [sbuf.tile([PART, L_TILES], F32, name="e_recip%d" % b) for b in range(CLIPS)]
@@ -125,10 +129,11 @@ def tile_stnonlocalgnlstage_pb_kernel(tc, att_logits, g, w1_w, w1_b, w2_w, w2_b,
         load_g(0)
         for half in range(2):
             load_att(1, half)
-        for i, w in enumerate((w1_w, w2_w)):
-            for half in range(2):
-                load_w(i, w, half)
+        for half in range(2):
+            load_w(0, w1_w, half)
         load_g(1)
+        for half in range(2):
+            load_w(1, w2_w, half)
         nc.sync.dma_start(out=b1[:], in_=w1_b.rearrange("(i ct) -> i ct", ct=C_TILES))
         nc.sync.dma_start(out=b2[:], in_=w2_b.rearrange("(i ct) -> i ct", ct=C_TILES))
 
@@ -154,6 +159,17 @@ def tile_stnonlocalgnlstage_pb_kernel(tc, att_logits, g, w1_w, w1_b, w2_w, w2_b,
                 out=neg_max[b][:, lt : lt + 1], in_=att_rows[b][:, lt, :], axis=AXIS.X, op=ALU.max, negate=True
             )
 
+        def fold_columns(b):
+            nc.vector.tensor_tensor(
+                out=fold_2[:], in0=att_rows[b][:, :, :HALF], in1=att_rows[b][:, :, HALF:], op=ALU.max
+            )
+
+        def fold_again():
+            nc.vector.tensor_tensor(out=fold_4[:], in0=fold_2[:, :, :PART], in1=fold_2[:, :, PART:], op=ALU.max)
+
+        def row_max_of_folded(b):
+            nc.vector.tensor_reduce(out=neg_max[b][:], in_=fold_4[:], axis=AXIS.X, op=ALU.max, negate=True)
+
         def exponential(b, lt):
             nc.scalar.activation(
                 out=e_rows[b][:, cols(lt, POSITIONS)],
@@ -172,14 +188,27 @@ def tile_stnonlocalgnlstage_pb_kernel(tc, att_logits, g, w1_w, w1_b, w2_w, w2_b,
                 )
             return acc
 
-        def regroup_g(b):
+        def regroup_g_vector(b):
             nc.vector.tensor_copy(
                 out=g_by_p[b]["values"][:].rearrange("q (c i t) -> q c t i", i=4, t=PACK),
                 in_=g_rows[b][:].rearrange("q (t c i) -> q c t i", t=PACK, i=4),
             )
 
+        def regroup_g_gpsimd(b):
+            for piece in range(L_TILES):
+                nc.gpsimd.tensor_scalar(
+                    out=g_by_p[b]["values"][:, cols(piece, PACK * PART)].rearrange("q (c i t) -> q c t i", i=4, t=PACK),
+                    in0=g_rows[b][:].rearrange("q (t m) -> q t m", t=PACK)[:, :, cols(piece, PART)].rearrange(
+                        "q t (c i) -> q c t i", i=4
+                    ),
+                    scalar1=1.0,
+                    scalar2=0.0,
+                    op0=ALU.mult,
+                    op1=ALU.add,
+                )
+
         def aggregate_multiply(b, lt):
-            acc = bank([PART, PACK, PART], F32, "y")
+            acc = bank([PART, PACK, PART], F32, "y%d" % b)
             for t in range(PACK):
                 multiply(acc[:, t, :], g_by_m[b], t, e_by_m[b], lt, PART, True, True)
             return acc
@@ -213,12 +242,10 @@ def tile_stnonlocalgnlstage_pb_kernel(tc, att_logits, g, w1_w, w1_b, w2_w, w2_b,
                     bias=bias[:, ct : ct + 1],
                     scale=1.0,
                 )
-            if ct % 2 == 1:
-                out_rows = out[b].rearrange("(i ct) l -> i ct l", ct=C_TILES)
-                nc.sync.dma_start(
-                    out=out_rows[:, ct - 1 : ct + 1, cols(piece, width)],
-                    in_=result[b][:, ct - 1 : ct + 1, cols(piece, width)],
-                )
+
+        def store(b, ct):
+            out_rows = out[b].rearrange("(i ct) l -> i ct l", ct=C_TILES)
+            nc.sync.dma_start(out=out_rows[:, ct : ct + 2, :], in_=result[b][:, ct : ct + 2, :])
 
         def keep_busy(times, width):
             acc = bank([PART, POSITIONS], F32, "unread")
@@ -231,6 +258,8 @@ def tile_stnonlocalgnlstage_pb_kernel(tc, att_logits, g, w1_w, w1_b, w2_w, w2_b,
             acc = project_g(b, ct, piece, width)
             project_y(b, ct, piece, width, acc)
             leave(b, ct, piece, width, acc, on_vector)
+            if ct % 2 == 1:
+                store(b, ct - 1)
 
         vector_copy, scalar_copy = nc.vector.tensor_copy, nc.scalar.copy
         half_channels = CHANNELS // 2
@@ -243,19 +272,19 @@ def tile_stnonlocalgnlstage_pb_kernel(tc, att_logits, g, w1_w, w1_b, w2_w, w2_b,
         for pair in range(2):
             turn(g_rows[0], g_by_m[0], pair, scalar_copy)
             keep_busy(1, HALF)
-        regroup_g(0)
-        row_max(1, 0)
-        row_max(1, 1)
+        regroup_g_vector(0)
+        fold_columns(1)
         for pair in range(2):
             turn(e_rows[0], e_by_m[0], pair, scalar_copy)
             keep_busy(1, POSITIONS)
+        quantise(g_by_p[0], 0, POSITIONS)
+        fold_again()
         nc.vector.reciprocal(out=e_recip[0][:], in_=e_sum[0][:])
         nc.scalar.copy(out=recip_rows[0][:], in_=spread_recip(0)[:])
-        quantise(g_by_p[0], 0, POSITIONS)
         quantise(g_by_m[0], 0, FEATURES)
+        row_max_of_folded(1)
         for pair in range(2):
             quantise(e_by_m[0], pair, 2 * PART)
-        row_max(1, 2)
 
         for pair in range(2):
             turn(w_rows[0], w_by_p[0], pair, scalar_copy)
@@ -264,54 +293,56 @@ def tile_stnonlocalgnlstage_pb_kernel(tc, att_logits, g, w1_w, w1_b, w2_w, w2_b,
         exponential(1, 0)
         exponential(1, 1)
         aggregate_divide(0, 0, y_banks[0])
-        row_max(1, 3)
-        for pair in range(2, 4):
-            turn(w_rows[0], w_by_p[0], pair, scalar_copy)
-            keep_busy(1, HALF)
-        y_banks += [aggregate_multiply(0, lt) for lt in range(2, 4)]
-        exponential(1, 2)
-        exponential(1, 3)
+        y_banks += [aggregate_multiply(0, 2)]
+        turn(w_rows[0], w_by_p[0], 2, scalar_copy)
+        keep_busy(1, HALF)
+        y_banks += [aggregate_multiply(0, 3)]
+        turn(w_rows[0], w_by_p[0], 3, scalar_copy)
+        keep_busy(1, HALF)
+        regroup_g_gpsimd(1)
+        nc.gpsimd.tensor_tensor(out=bias[:], in0=b1[:], in1=b2[:], op=ALU.add)
         for lt in range(1, L_TILES):
             aggregate_divide(0, lt, y_banks[lt])
-            quantise(y_by_p[0], lt - 1, PART)
 
         for pair in range(2):
             turn(w_rows[1], w_by_p[1], pair, scalar_copy)
             keep_busy(1, HALF)
+        exponential(1, 2)
+        exponential(1, 3)
+        g_banks = [transpose_words(g_rows[1], pair) for pair in range(2)]
+        keep_busy(1, POSITIONS)
+        e_banks = [transpose_words(e_rows[1], 0, "e1")]
         quantise(w_by_p[0], 0, half_channels)
-        quantise(y_by_p[0], L_TILES - 1, PART)
-        quantise(w_by_p[0], 1, half_channels)
-        e_banks = [transpose_words(e_rows[1], 0, "y")]
-        nc.vector.reciprocal(out=e_recip[1][:], in_=e_sum[1][:])
+        quantise(y_by_p[0], 0, POSITIONS)
+        for pair in range(2):
+            copy_words(g_banks[pair], g_by_m[1], pair, vector_copy)
+        quantise(w_by_p[1], 0, half_channels)
+        first_banks = [project_g(0, ct, 0, POSITIONS) for ct in range(2)]
         for pair in range(2, 4):
             turn(w_rows[1], w_by_p[1], pair, scalar_copy)
-            keep_busy(1, HALF)
-        quantise(w_by_p[1], 0, half_channels)
-        e_banks += [transpose_words(e_rows[1], 1, "y")]
-        turn(g_rows[1], g_by_m[1], 0, scalar_copy)
-        turn(g_rows[1], g_by_m[1], 1, vector_copy)
+        e_banks += [transpose_words(e_rows[1], 1, "e1")]
+        quantise(w_by_p[0], 1, half_channels)
+        nc.vector.reciprocal(out=e_recip[1][:], in_=e_sum[1][:])
+        quantise(g_by_m[1], 0, FEATURES)
         copy_words(e_banks[0], e_by_m[1], 0, scalar_copy)
         quantise(w_by_p[1], 1, half_channels)
-        nc.vector.tensor_tensor(out=bias[:], in0=b1[:], in1=b2[:], op=ALU.add)
-        recip_bank = spread_recip(1)
-
-        first_banks = [project_g(0, ct, 0, POSITIONS) for ct in range(2)]
         for ct in range(2):
             project_y(0, ct, 0, POSITIONS, first_banks[ct])
+        recip_bank = spread_recip(1)
         for ct in range(2):
             leave(0, ct, 0, POSITIONS, first_banks[ct], False)
-        quantise(g_by_m[1], 0, FEATURES)
+        store(0, 0)
+        store(0, 0)
         quantise(e_by_m[1], 0, 2 * PART)
         copy_words(e_banks[1], e_by_m[1], 1, scalar_copy)
         nc.scalar.copy(out=recip_rows[1][:], in_=recip_bank[:])
-        regroup_g(1)
+        quantise(g_by_p[1], 0, POSITIONS)
         quantise(e_by_m[1], 1, 2 * PART)
         for ct in range(2, 4):
             project(0, ct, 0, POSITIONS, False)
         y_banks = [aggregate_multiply(1, lt) for lt in range(2)]
         for lt in range(2):
             aggregate_divide(1, lt, y_banks[lt])
-        quantise(g_by_p[1], 0, POSITIONS)
         quantise(y_by_p[1], 0, PART)
         for ct in range(4, 6):
             project(0, ct, 0, POSITIONS, False)
@@ -323,13 +354,17 @@ def tile_stnonlocalgnlstage_pb_kernel(tc, att_logits, g, w1_w, w1_b, w2_w, w2_b,
             quantise(y_by_p[1], lt - 1, PART)
         quantise(y_by_p[1], L_TILES - 1, PART)
 
-        tiles = [(piece, ct) for piece in range(2) for ct in range(C_TILES)]
+        units = [(ct, piece, HALF) for piece in range(2) for ct in range(C_TILES // 2)]
+        units += [(ct, 0, POSITIONS) for ct in range(C_TILES // 2, C_TILES)]
+        ahead = 2
         banks = []
-        for i in range(len(tiles) + 4):
-            if i < len(tiles):
-                piece, ct = tiles[i]
-                banks.append(project_g(1, ct, piece, HALF))
-            if i >= 4:
-                piece, ct = tiles[i - 4]
-                project_y(1, ct, piece, HALF, banks[i - 4])
-                leave(1, ct, piece, HALF, banks[i - 4], ct % 2 == 1)
+        for i in range(len(units) + ahead):
+            if i < len(units):
+                ct, piece, width = units[i]
+                banks.append(project_g(1, ct, piece, width))
+            if i >= ahead:
+                ct, piece, width = units[i - ahead]
+                project_y(1, ct, piece, width, banks[i - ahead])
+                leave(1, ct, piece, width, banks[i - ahead], i % 2 == 1)
+                if ct % 2 == 1 and (piece + 1) * width == POSITIONS:
+                    store(1, ct - 1)

@@ -129,9 +129,9 @@ def tile_stnonlocalgnlstage_pb_kernel(tc, att_logits, g, w1_w, w1_b, w2_w, w2_b,
         load_g(0)
         for half in range(2):
             load_att(1, half)
-        for half in range(2):
-            load_w(0, w1_w, half)
+        load_w(0, w1_w, 0)
         load_g(1)
+        load_w(0, w1_w, 1)
         for half in range(2):
             load_w(1, w2_w, half)
         nc.sync.dma_start(out=b1[:], in_=w1_b.rearrange("(i ct) -> i ct", ct=C_TILES))
@@ -242,10 +242,12 @@ def tile_stnonlocalgnlstage_pb_kernel(tc, att_logits, g, w1_w, w1_b, w2_w, w2_b,
                     bias=bias[:, ct : ct + 1],
                     scale=1.0,
                 )
-
-        def store(b, ct):
-            out_rows = out[b].rearrange("(i ct) l -> i ct l", ct=C_TILES)
-            nc.sync.dma_start(out=out_rows[:, ct : ct + 2, :], in_=result[b][:, ct : ct + 2, :])
+            if ct % 2 == 1:
+                out_rows = out[b].rearrange("(i ct) l -> i ct l", ct=C_TILES)
+                nc.sync.dma_start(
+                    out=out_rows[:, ct - 1 : ct + 1, cols(piece, width)],
+                    in_=result[b][:, ct - 1 : ct + 1, cols(piece, width)],
+                )
 
         def keep_busy(times, width):
             acc = bank([PART, POSITIONS], F32, "unread")
@@ -258,8 +260,6 @@ def tile_stnonlocalgnlstage_pb_kernel(tc, att_logits, g, w1_w, w1_b, w2_w, w2_b,
             acc = project_g(b, ct, piece, width)
             project_y(b, ct, piece, width, acc)
             leave(b, ct, piece, width, acc, on_vector)
-            if ct % 2 == 1:
-                store(b, ct - 1)
 
         vector_copy, scalar_copy = nc.vector.tensor_copy, nc.scalar.copy
         half_channels = CHANNELS // 2
@@ -273,27 +273,26 @@ def tile_stnonlocalgnlstage_pb_kernel(tc, att_logits, g, w1_w, w1_b, w2_w, w2_b,
             turn(g_rows[0], g_by_m[0], pair, scalar_copy)
             keep_busy(1, HALF)
         regroup_g_vector(0)
+        nc.vector.reciprocal(out=e_recip[0][:], in_=e_sum[0][:])
         fold_columns(1)
         for pair in range(2):
             turn(e_rows[0], e_by_m[0], pair, scalar_copy)
             keep_busy(1, POSITIONS)
         quantise(g_by_p[0], 0, POSITIONS)
         fold_again()
-        nc.vector.reciprocal(out=e_recip[0][:], in_=e_sum[0][:])
         nc.scalar.copy(out=recip_rows[0][:], in_=spread_recip(0)[:])
         quantise(g_by_m[0], 0, FEATURES)
-        row_max_of_folded(1)
         for pair in range(2):
             quantise(e_by_m[0], pair, 2 * PART)
+        row_max_of_folded(1)
 
         for pair in range(2):
             turn(w_rows[0], w_by_p[0], pair, scalar_copy)
             keep_busy(1, HALF)
-        y_banks = [aggregate_multiply(0, lt) for lt in range(2)]
         exponential(1, 0)
         exponential(1, 1)
+        y_banks = [aggregate_multiply(0, lt) for lt in range(3)]
         aggregate_divide(0, 0, y_banks[0])
-        y_banks += [aggregate_multiply(0, 2)]
         turn(w_rows[0], w_by_p[0], 2, scalar_copy)
         keep_busy(1, HALF)
         y_banks += [aggregate_multiply(0, 3)]
@@ -314,26 +313,24 @@ def tile_stnonlocalgnlstage_pb_kernel(tc, att_logits, g, w1_w, w1_b, w2_w, w2_b,
         e_banks = [transpose_words(e_rows[1], 0, "e1")]
         quantise(w_by_p[0], 0, half_channels)
         quantise(y_by_p[0], 0, POSITIONS)
-        for pair in range(2):
-            copy_words(g_banks[pair], g_by_m[1], pair, vector_copy)
         quantise(w_by_p[1], 0, half_channels)
+        turn(w_rows[1], w_by_p[1], 2, scalar_copy)
         first_banks = [project_g(0, ct, 0, POSITIONS) for ct in range(2)]
-        for pair in range(2, 4):
-            turn(w_rows[1], w_by_p[1], pair, scalar_copy)
-        e_banks += [transpose_words(e_rows[1], 1, "e1")]
-        quantise(w_by_p[0], 1, half_channels)
-        nc.vector.reciprocal(out=e_recip[1][:], in_=e_sum[1][:])
-        quantise(g_by_m[1], 0, FEATURES)
-        copy_words(e_banks[0], e_by_m[1], 0, scalar_copy)
-        quantise(w_by_p[1], 1, half_channels)
         for ct in range(2):
             project_y(0, ct, 0, POSITIONS, first_banks[ct])
+        for pair in range(2):
+            copy_words(g_banks[pair], g_by_m[1], pair, vector_copy)
+        copy_words(e_banks[0], e_by_m[1], 0, scalar_copy)
+        leave(0, 0, 0, POSITIONS, first_banks[0], False)
+        turn(w_rows[1], w_by_p[1], 3, scalar_copy)
+        e_banks += [transpose_words(e_rows[1], 1, "e1")]
+        nc.vector.reciprocal(out=e_recip[1][:], in_=e_sum[1][:])
         recip_bank = spread_recip(1)
-        for ct in range(2):
-            leave(0, ct, 0, POSITIONS, first_banks[ct], False)
-        store(0, 0)
-        store(0, 0)
+        quantise(w_by_p[0], 1, half_channels)
+        quantise(g_by_m[1], 0, FEATURES)
+        leave(0, 1, 0, POSITIONS, first_banks[1], False)
         quantise(e_by_m[1], 0, 2 * PART)
+        quantise(w_by_p[1], 1, half_channels)
         copy_words(e_banks[1], e_by_m[1], 1, scalar_copy)
         nc.scalar.copy(out=recip_rows[1][:], in_=recip_bank[:])
         quantise(g_by_p[1], 0, POSITIONS)
@@ -354,17 +351,13 @@ def tile_stnonlocalgnlstage_pb_kernel(tc, att_logits, g, w1_w, w1_b, w2_w, w2_b,
             quantise(y_by_p[1], lt - 1, PART)
         quantise(y_by_p[1], L_TILES - 1, PART)
 
-        units = [(ct, piece, HALF) for piece in range(2) for ct in range(C_TILES // 2)]
-        units += [(ct, 0, POSITIONS) for ct in range(C_TILES // 2, C_TILES)]
-        ahead = 2
+        tiles = [(piece, ct) for piece in range(2) for ct in range(C_TILES)]
         banks = []
-        for i in range(len(units) + ahead):
-            if i < len(units):
-                ct, piece, width = units[i]
-                banks.append(project_g(1, ct, piece, width))
-            if i >= ahead:
-                ct, piece, width = units[i - ahead]
-                project_y(1, ct, piece, width, banks[i - ahead])
-                leave(1, ct, piece, width, banks[i - ahead], i % 2 == 1)
-                if ct % 2 == 1 and (piece + 1) * width == POSITIONS:
-                    store(1, ct - 1)
+        for i in range(len(tiles) + 3):
+            if i < len(tiles):
+                piece, ct = tiles[i]
+                banks.append(project_g(1, ct, piece, HALF))
+            if i >= 3:
+                piece, ct = tiles[i - 3]
+                project_y(1, ct, piece, HALF, banks[i - 3])
+                leave(1, ct, piece, HALF, banks[i - 3], ct % 2 == 1)

@@ -294,10 +294,8 @@ def tile_stnonlocalgnlstage_pb_kernel(tc, att_logits, g, w1_w, w1_b, w2_w, w2_b,
         y_banks = [aggregate_multiply(0, lt) for lt in range(3)]
         aggregate_divide(0, 0, y_banks[0])
         turn(w_rows[0], w_by_p[0], 2, scalar_copy)
-        keep_busy(1, HALF)
         y_banks += [aggregate_multiply(0, 3)]
         turn(w_rows[0], w_by_p[0], 3, scalar_copy)
-        keep_busy(1, HALF)
         regroup_g_gpsimd(1)
         nc.gpsimd.tensor_tensor(out=bias[:], in0=b1[:], in1=b2[:], op=ALU.add)
         for lt in range(1, L_TILES):
@@ -305,11 +303,9 @@ def tile_stnonlocalgnlstage_pb_kernel(tc, att_logits, g, w1_w, w1_b, w2_w, w2_b,
 
         for pair in range(2):
             turn(w_rows[1], w_by_p[1], pair, scalar_copy)
-            keep_busy(1, HALF)
         exponential(1, 2)
         exponential(1, 3)
         g_banks = [transpose_words(g_rows[1], pair) for pair in range(2)]
-        keep_busy(1, POSITIONS)
         e_banks = [transpose_words(e_rows[1], 0, "e1")]
         quantise(w_by_p[0], 0, half_channels)
         quantise(y_by_p[0], 0, POSITIONS)

@@ -242,12 +242,10 @@ def tile_stnonlocalgnlstage_pb_kernel(tc, att_logits, g, w1_w, w1_b, w2_w, w2_b,
                     bias=bias[:, ct : ct + 1],
                     scale=1.0,
                 )
-            if ct % 2 == 1:
-                out_rows = out[b].rearrange("(i ct) l -> i ct l", ct=C_TILES)
-                nc.sync.dma_start(
-                    out=out_rows[:, ct - 1 : ct + 1, cols(piece, width)],
-                    in_=result[b][:, ct - 1 : ct + 1, cols(piece, width)],
-                )
+
+        def store(b, ct, n=2):
+            out_rows = out[b].rearrange("(i ct) l -> i ct l", ct=C_TILES)
+            nc.sync.dma_start(out=out_rows[:, ct : ct + n, :], in_=result[b][:, ct : ct + n, :])
 
         def keep_busy(times, width):
             acc = bank([PART, POSITIONS], F32, "unread")
@@ -260,6 +258,8 @@ def tile_stnonlocalgnlstage_pb_kernel(tc, att_logits, g, w1_w, w1_b, w2_w, w2_b,
             acc = project_g(b, ct, piece, width)
             project_y(b, ct, piece, width, acc)
             leave(b, ct, piece, width, acc, on_vector)
+            if ct % 2 == 1:
+                store(b, ct - 1)
 
         vector_copy, scalar_copy = nc.vector.tensor_copy, nc.scalar.copy
         half_channels = CHANNELS // 2
@@ -325,6 +325,7 @@ def tile_stnonlocalgnlstage_pb_kernel(tc, att_logits, g, w1_w, w1_b, w2_w, w2_b,
         quantise(w_by_p[0], 1, half_channels)
         quantise(g_by_m[1], 0, FEATURES)
         leave(0, 1, 0, POSITIONS, first_banks[1], False)
+        store(0, 0)
         quantise(e_by_m[1], 0, 2 * PART)
         quantise(w_by_p[1], 1, half_channels)
         copy_words(e_banks[1], e_by_m[1], 1, scalar_copy)
@@ -347,13 +348,17 @@ def tile_stnonlocalgnlstage_pb_kernel(tc, att_logits, g, w1_w, w1_b, w2_w, w2_b,
             quantise(y_by_p[1], lt - 1, PART)
         quantise(y_by_p[1], L_TILES - 1, PART)
 
-        tiles = [(piece, ct) for piece in range(2) for ct in range(C_TILES)]
+        units = [(ct, piece, HALF) for piece in range(2) for ct in range(2)]
+        units += [(ct, 0, POSITIONS) for ct in range(2, C_TILES)]
+        ahead = 1
         banks = []
-        for i in range(len(tiles) + 3):
-            if i < len(tiles):
-                piece, ct = tiles[i]
-                banks.append(project_g(1, ct, piece, HALF))
-            if i >= 3:
-                piece, ct = tiles[i - 3]
-                project_y(1, ct, piece, HALF, banks[i - 3])
-                leave(1, ct, piece, HALF, banks[i - 3], ct % 2 == 1)
+        for i in range(len(units) + ahead):
+            if i < len(units):
+                ct, piece, width = units[i]
+                banks.append(project_g(1, ct, piece, width))
+            if i >= ahead:
+                ct, piece, width = units[i - ahead]
+                project_y(1, ct, piece, width, banks[i - ahead])
+                leave(1, ct, piece, width, banks[i - ahead], i % 2 == 1)
+                if (piece + 1) * width == POSITIONS:
+                    store(1, ct, 1)

@@ -131,9 +131,9 @@ def tile_stnonlocalgnlstage_pb_kernel(tc, att_logits, g, w1_w, w1_b, w2_w, w2_b,
             load_att(1, half)
         load_w(0, w1_w, 0)
         load_g(1)
+        load_w(1, w2_w, 0)
         load_w(0, w1_w, 1)
-        for half in range(2):
-            load_w(1, w2_w, half)
+        load_w(1, w2_w, 1)
         nc.sync.dma_start(out=b1[:], in_=w1_b.rearrange("(i ct) -> i ct", ct=C_TILES))
         nc.sync.dma_start(out=b2[:], in_=w2_b.rearrange("(i ct) -> i ct", ct=C_TILES))
 
@@ -258,7 +258,9 @@ def tile_stnonlocalgnlstage_pb_kernel(tc, att_logits, g, w1_w, w1_b, w2_w, w2_b,
             acc = project_g(b, ct, piece, width)
             project_y(b, ct, piece, width, acc)
             leave(b, ct, piece, width, acc, on_vector)
-            if ct % 2 == 1:
+            if ct < 8:
+                store(b, ct, 1)
+            elif ct % 2 == 1:
                 store(b, ct - 1)
 
         vector_copy, scalar_copy = nc.vector.tensor_copy, nc.scalar.copy
@@ -293,44 +295,44 @@ def tile_stnonlocalgnlstage_pb_kernel(tc, att_logits, g, w1_w, w1_b, w2_w, w2_b,
         exponential(1, 1)
         y_banks = [aggregate_multiply(0, lt) for lt in range(3)]
         aggregate_divide(0, 0, y_banks[0])
-        turn(w_rows[0], w_by_p[0], 2, scalar_copy)
+        turn(w_rows[1], w_by_p[1], 0, scalar_copy)
         y_banks += [aggregate_multiply(0, 3)]
-        turn(w_rows[0], w_by_p[0], 3, scalar_copy)
+        turn(w_rows[1], w_by_p[1], 1, scalar_copy)
         regroup_g_gpsimd(1)
         nc.gpsimd.tensor_tensor(out=bias[:], in0=b1[:], in1=b2[:], op=ALU.add)
         for lt in range(1, L_TILES):
             aggregate_divide(0, lt, y_banks[lt])
 
-        for pair in range(2):
-            turn(w_rows[1], w_by_p[1], pair, scalar_copy)
+        for pair in range(2, 4):
+            turn(w_rows[0], w_by_p[0], pair, scalar_copy)
         exponential(1, 2)
         exponential(1, 3)
-        g_banks = [transpose_words(g_rows[1], pair) for pair in range(2)]
-        e_banks = [transpose_words(e_rows[1], 0, "e1")]
         quantise(w_by_p[0], 0, half_channels)
         quantise(y_by_p[0], 0, POSITIONS)
+        g_banks = [transpose_words(g_rows[1], pair) for pair in range(2)]
+        first_banks = [project_g(0, ct, 0, POSITIONS) for ct in range(2)]
+        e_banks = [transpose_words(e_rows[1], 0, "e1")]
         quantise(w_by_p[1], 0, half_channels)
         turn(w_rows[1], w_by_p[1], 2, scalar_copy)
-        first_banks = [project_g(0, ct, 0, POSITIONS) for ct in range(2)]
         for ct in range(2):
             project_y(0, ct, 0, POSITIONS, first_banks[ct])
         for pair in range(2):
             copy_words(g_banks[pair], g_by_m[1], pair, vector_copy)
         copy_words(e_banks[0], e_by_m[1], 0, scalar_copy)
         leave(0, 0, 0, POSITIONS, first_banks[0], False)
+        store(0, 0, 1)
         turn(w_rows[1], w_by_p[1], 3, scalar_copy)
         e_banks += [transpose_words(e_rows[1], 1, "e1")]
         nc.vector.reciprocal(out=e_recip[1][:], in_=e_sum[1][:])
-        recip_bank = spread_recip(1)
+        nc.scalar.copy(out=recip_rows[1][:], in_=spread_recip(1)[:])
         quantise(w_by_p[0], 1, half_channels)
         quantise(g_by_m[1], 0, FEATURES)
-        leave(0, 1, 0, POSITIONS, first_banks[1], False)
-        store(0, 0)
-        quantise(e_by_m[1], 0, 2 * PART)
-        quantise(w_by_p[1], 1, half_channels)
         copy_words(e_banks[1], e_by_m[1], 1, scalar_copy)
-        nc.scalar.copy(out=recip_rows[1][:], in_=recip_bank[:])
+        quantise(e_by_m[1], 0, 2 * PART)
         quantise(g_by_p[1], 0, POSITIONS)
+        quantise(w_by_p[1], 1, half_channels)
+        leave(0, 1, 0, POSITIONS, first_banks[1], True)
+        store(0, 1, 1)
         quantise(e_by_m[1], 1, 2 * PART)
         for ct in range(2, 4):
             project(0, ct, 0, POSITIONS, False)

@@ -243,6 +243,12 @@ def tile_stnonlocalgnlstage_pb_kernel(tc, att_logits, g, w1_w, w1_b, w2_w, w2_b,
                     scale=1.0,
                 )
 
+        def store_piece(b, ct, piece, width):
+            out_rows = out[b].rearrange("(i ct) l -> i ct l", ct=C_TILES)
+            nc.sync.dma_start(
+                out=out_rows[:, ct, cols(piece, width)], in_=result[b][:, ct, cols(piece, width)]
+            )
+
         def store(b, ct, n=2):
             out_rows = out[b].rearrange("(i ct) l -> i ct l", ct=C_TILES)
             nc.sync.dma_start(out=out_rows[:, ct : ct + n, :], in_=result[b][:, ct : ct + n, :])
@@ -330,9 +336,9 @@ def tile_stnonlocalgnlstage_pb_kernel(tc, att_logits, g, w1_w, w1_b, w2_w, w2_b,
         copy_words(e_banks[1], e_by_m[1], 1, scalar_copy)
         quantise(e_by_m[1], 0, 2 * PART)
         quantise(g_by_p[1], 0, POSITIONS)
-        quantise(w_by_p[1], 1, half_channels)
         leave(0, 1, 0, POSITIONS, first_banks[1], True)
         store(0, 1, 1)
+        quantise(w_by_p[1], 1, half_channels)
         quantise(e_by_m[1], 1, 2 * PART)
         for ct in range(2, 4):
             project(0, ct, 0, POSITIONS, False)
@@ -351,7 +357,8 @@ def tile_stnonlocalgnlstage_pb_kernel(tc, att_logits, g, w1_w, w1_b, w2_w, w2_b,
         quantise(y_by_p[1], L_TILES - 1, PART)
 
         units = [(ct, piece, HALF) for piece in range(2) for ct in range(2)]
-        units += [(ct, 0, POSITIONS) for ct in range(2, C_TILES)]
+        units += [(ct, 0, POSITIONS) for ct in range(2, C_TILES - 1)]
+        units += [(ct, piece, HALF) for ct in range(C_TILES - 1, C_TILES) for piece in range(2)]
         ahead = 1
         banks = []
         for i in range(len(units) + ahead):
@@ -362,5 +369,7 @@ def tile_stnonlocalgnlstage_pb_kernel(tc, att_logits, g, w1_w, w1_b, w2_w, w2_b,
                 ct, piece, width = units[i - ahead]
                 project_y(1, ct, piece, width, banks[i - ahead])
                 leave(1, ct, piece, width, banks[i - ahead], i % 2 == 1)
-                if (piece + 1) * width == POSITIONS:
+                if ct >= C_TILES - 1:
+                    store_piece(1, ct, piece, width)
+                elif (piece + 1) * width == POSITIONS:
                     store(1, ct, 1)

@@ -25,12 +25,12 @@ C_TILES = CHANNELS // PART
 HALF = POSITIONS // 2
 BANKS = {
     "turned": (0, 1, 2, 3),
-    "y0": (4, 5, 6),
+    "y0": (4, 5, 6, 7),
     "e1": (5, 6),
     "unread": (7,),
-    "out0": (7, 4, 0, 1),
-    "y1": (5, 2, 6, 3),
-    "out1": (5, 2, 7, 4, 6, 0, 3, 1),
+    "out0": (7, 4, 0, 1, 7, 3, 0, 1),
+    "y1": (5, 2, 6, 4),
+    "out1": (5, 2, 7, 6, 3, 0, 4, 1),
 }
 
 FLOPS = 2 * CLIPS * (POSITIONS * POSITIONS * FEATURES + 2 * POSITIONS * FEATURES * CHANNELS)
@@ -287,11 +287,11 @@ def tile_stnonlocalgnlstage_pb_kernel(tc, att_logits, g, w1_w, w1_b, w2_w, w2_b,
             turn(e_rows[0], e_by_m[0], pair, scalar_copy)
             keep_busy(1, POSITIONS)
         quantise(g_by_p[0], 0, POSITIONS)
-        fold_again()
         nc.scalar.copy(out=recip_rows[0][:], in_=spread_recip(0)[:])
         quantise(g_by_m[0], 0, FEATURES)
-        for pair in range(2):
-            quantise(e_by_m[0], pair, 2 * PART)
+        quantise(e_by_m[0], 0, 2 * PART)
+        fold_again()
+        quantise(e_by_m[0], 1, 2 * PART)
         row_max_of_folded(1)
 
         for pair in range(2):
@@ -299,10 +299,9 @@ def tile_stnonlocalgnlstage_pb_kernel(tc, att_logits, g, w1_w, w1_b, w2_w, w2_b,
             keep_busy(1, HALF)
         exponential(1, 0)
         exponential(1, 1)
-        y_banks = [aggregate_multiply(0, lt) for lt in range(3)]
+        y_banks = [aggregate_multiply(0, lt) for lt in range(L_TILES)]
         aggregate_divide(0, 0, y_banks[0])
         turn(w_rows[1], w_by_p[1], 0, scalar_copy)
-        y_banks += [aggregate_multiply(0, 3)]
         turn(w_rows[1], w_by_p[1], 1, scalar_copy)
         regroup_g_gpsimd(1)
         nc.gpsimd.tensor_tensor(out=bias[:], in0=b1[:], in1=b2[:], op=ALU.add)
@@ -316,10 +315,10 @@ def tile_stnonlocalgnlstage_pb_kernel(tc, att_logits, g, w1_w, w1_b, w2_w, w2_b,
         quantise(w_by_p[0], 0, half_channels)
         quantise(y_by_p[0], 0, POSITIONS)
         g_banks = [transpose_words(g_rows[1], pair) for pair in range(2)]
-        first_banks = [project_g(0, ct, 0, POSITIONS) for ct in range(2)]
         e_banks = [transpose_words(e_rows[1], 0, "e1")]
         quantise(w_by_p[1], 0, half_channels)
         turn(w_rows[1], w_by_p[1], 2, scalar_copy)
+        first_banks = [project_g(0, ct, 0, POSITIONS) for ct in range(2)]
         for ct in range(2):
             project_y(0, ct, 0, POSITIONS, first_banks[ct])
         for pair in range(2):
@@ -336,9 +335,9 @@ def tile_stnonlocalgnlstage_pb_kernel(tc, att_logits, g, w1_w, w1_b, w2_w, w2_b,
         copy_words(e_banks[1], e_by_m[1], 1, scalar_copy)
         quantise(e_by_m[1], 0, 2 * PART)
         quantise(g_by_p[1], 0, POSITIONS)
+        quantise(w_by_p[1], 1, half_channels)
         leave(0, 1, 0, POSITIONS, first_banks[1], True)
         store(0, 1, 1)
-        quantise(w_by_p[1], 1, half_channels)
         quantise(e_by_m[1], 1, 2 * PART)
         for ct in range(2, 4):
             project(0, ct, 0, POSITIONS, False)
@@ -356,8 +355,8 @@ def tile_stnonlocalgnlstage_pb_kernel(tc, att_logits, g, w1_w, w1_b, w2_w, w2_b,
             quantise(y_by_p[1], lt - 1, PART)
         quantise(y_by_p[1], L_TILES - 1, PART)
 
-        units = [(ct, piece, HALF) for piece in range(2) for ct in range(2)]
-        units += [(ct, 0, POSITIONS) for ct in range(2, C_TILES - 1)]
+        units = [(ct, piece, HALF) for piece in range(2) for ct in range(3)]
+        units += [(ct, 0, POSITIONS) for ct in range(3, C_TILES - 1)]
         units += [(ct, piece, HALF) for ct in range(C_TILES - 1, C_TILES) for piece in range(2)]
         ahead = 1
         banks = []

from contextlib import ExitStack

import concourse.masks as masks
import concourse.mybir as mybir

BF16 = mybir.dt.bfloat16
F32 = mybir.dt.float32
U32 = mybir.dt.uint32
U8 = mybir.dt.uint8
FP8X4 = mybir.dt.float8_e4m3fn_x4
ACT = mybir.ActivationFunctionType
ALU = mybir.AluOpType
AXIS = mybir.AxisListType

CLIPS = 2
POSITIONS = 512
FEATURES = 512
CHANNELS = 1024

PART = 128
PACK = 4
L_TILES = POSITIONS // PART
P_TILES = FEATURES // PART
C_TILES = CHANNELS // PART
HALF = POSITIONS // 2
BANKS = {
    "turned": (0, 1, 2, 3),
    "y0": (4, 5, 6, 7),
    "e1": (5, 6),
    "unread": (7,),
    "out0": (7, 4, 0, 1, 7, 3, 0, 1),
    "y1": (5, 2, 6, 4),
    "out1": (5, 2, 7, 6, 3, 0, 4, 1),
}

FLOPS = 2 * CLIPS * (POSITIONS * POSITIONS * FEATURES + 2 * POSITIONS * FEATURES * CHANNELS)


def cols(i, width):
    return slice(i * width, (i + 1) * width)


def tile_stnonlocalgnlstage_pb_kernel(tc, att_logits, g, w1_w, w1_b, w2_w, w2_b, out):
    nc = tc.nc
    with ExitStack() as ctx:
        sbuf = ctx.enter_context(tc.tile_pool(name="sbuf", bufs=1))
        psum = ctx.enter_context(tc.psum_pool(name="psum", bufs=1))
        ctx.enter_context(tc.manual_schedule())

        turns = {}

        def bank(shape, dtype, use):
            turns[use] = turns.get(use, -1) + 1
            tag = "bank%d" % BANKS[use][turns[use] % len(BANKS[use])]
            return psum.tile(shape, dtype, name=tag, tag=tag)

        def mx_operand(name, n_cols):
            return {
                "values": sbuf.tile([PART, n_cols * PACK], BF16, name=name + "_values", align_bytes=64),
                "codes": sbuf.tile([PART, n_cols], U32, name=name + "_codes", align_bytes=64),
                "scales": sbuf.tile([PART, n_cols], U8, name=name + "_scales", align_bytes=64),
            }

        def quantise(operand, piece, width):
            nc.vector.quantize_mx(
                out=operand["codes"][:, cols(piece, width)].bitcast(FP8X4),
                scales=operand["scales"][:, cols(piece, width)],
                in_=operand["values"][:, cols(piece, PACK * width)],
            )

        def multiply(acc, stationary, s_piece, moving, m_piece, m_width, start, stop):
            nc.tensor.matmul_mx(
                out=acc,
                lhsT=stationary["codes"][:, cols(s_piece, PART)].bitcast(FP8X4),
                lhsT_scale=stationary["scales"][:, cols(s_piece, PART)],
                rhs=moving["codes"][:, cols(m_piece, m_width)].bitcast(FP8X4),
                rhs_scale=moving["scales"][:, cols(m_piece, m_width)],
                start=start,
                stop=stop,
            )

        ident_f32 = sbuf.tile([PART, PART], F32)
        masks.make_identity(nc, ident_f32[:])

        warm = sbuf.tile([PART, 1], F32)
        nc.vector.memset(warm[:], 0.0)
        nc.scalar.activation(out=warm[:], in_=warm[:], func=ACT.Exp)

        att_rows = [sbuf.tile([PART, L_TILES, POSITIONS], BF16, name="att_rows%d" % b) for b in range(CLIPS)]
        g_rows = [sbuf.tile([PART, PACK * POSITIONS], BF16, name="g_rows%d" % b) for b in range(CLIPS)]
        w_rows = [sbuf.tile([PART, C_TILES * FEATURES], BF16, name="w_rows%d" % i) for i in range(2)]
        b1 = sbuf.tile([PART, C_TILES], BF16)
        b2 = sbuf.tile([PART, C_TILES], BF16)
        bias = sbuf.tile([PART, C_TILES], F32)
        fold_2 = sbuf.tile([PART, L_TILES, HALF], BF16)
        fold_4 = sbuf.tile([PART, L_TILES, PART], BF16)
        neg_max = [sbuf.tile([PART, L_TILES], F32, name="neg_max%d" % b) for b in range(CLIPS)]
        e_sum = [sbuf.tile([PART, L_TILES], F32, name="e_sum%d" % b) for b in range(CLIPS)]
        e_recip = [sbuf.tile([PART, L_TILES], F32, name="e_recip%d" % b) for b in range(CLIPS)]
        e_rows = [sbuf.tile([PART, L_TILES * POSITIONS], BF16, name="e_rows%d" % b) for b in range(CLIPS)]
        recip_rows = [sbuf.tile([PART, POSITIONS], F32, name="recip_rows%d" % b) for b in range(CLIPS)]
        result = [sbuf.tile([PART, C_TILES, POSITIONS], F32, name="result%d" % b) for b in range(CLIPS)]
        e_by_m = [mx_operand("e_by_m%d" % b, POSITIONS) for b in range(CLIPS)]
        g_by_m = [mx_operand("g_by_m%d" % b, FEATURES) for b in range(CLIPS)]
        g_by_p = [mx_operand("g_by_p%d" % b, POSITIONS) for b in range(CLIPS)]
        y_by_p = [mx_operand("y_by_p%d" % b, POSITIONS) for b in range(CLIPS)]
        w_by_p = [mx_operand("w_by_p%d" % i, CHANNELS) for i in range(2)]

        def load_g(b):
            nc.sync.dma_start(
                out=g_rows[b][:].rearrange("j (u e m) -> j u e m", u=2, e=2),
                in_=g[b].rearrange("(u j e) m -> j u e m", u=2, e=2),
            )

        def load_w(i, w, half):
            nc.sync.dma_start(
                out=w_rows[i][:, cols(half, C_TILES * FEATURES // 2)],
                in_=w.rearrange("(i ct) p -> i (ct p)", ct=C_TILES)[:, cols(half, C_TILES * FEATURES // 2)],
            )

        def load_att(b, half):
            nc.sync.dma_start(
                out=att_rows[b][:, cols(half, L_TILES // 2), :],
                in_=att_logits[b, cols(half, HALF), :].rearrange("(lt l) m -> l lt m", l=PART),
            )

        for lt in range(L_TILES):
            nc.sync.dma_start(out=att_rows[0][:, lt, :], in_=att_logits[0, cols(lt, PART), :])
        load_g(0)
        for half in range(2):
            load_att(1, half)
        load_w(0, w1_w, 0)
        load_g(1)
        load_w(1, w2_w, 0)
        load_w(0, w1_w, 1)
        load_w(1, w2_w, 1)
        nc.sync.dma_start(out=b1[:], in_=w1_b.rearrange("(i ct) -> i ct", ct=C_TILES))
        nc.sync.dma_start(out=b2[:], in_=w2_b.rearrange("(i ct) -> i ct", ct=C_TILES))

        def transpose_words(rows, pair, use="turned"):
            words = rows[:].bitcast(F32)
            acc = bank([PART, 2, 2, PART], F32, use)
            for n in range(2):
                for u in range(2):
                    nc.tensor.transpose(acc[:, n, u, :], words[:, cols(4 * pair + 2 * n + u, PART)], ident_f32[:])
            return acc

        def copy_words(acc, operand, pair, copy):
            copy(
                out=operand["values"][:].bitcast(F32)[:, cols(pair, 4 * PART)].rearrange("q (n r u) -> q n r u", n=2, u=2),
                in_=acc[:].rearrange("q n u r -> q n r u"),
            )

        def turn(rows, operand, pair, copy):
            copy_words(transpose_words(rows, pair), operand, pair, copy)

        def row_max(b, lt):
            nc.vector.tensor_reduce(
                out=neg_max[b][:, lt : lt + 1], in_=att_rows[b][:, lt, :], axis=AXIS.X, op=ALU.max, negate=True
            )

        def fold_columns(b):
            nc.vector.tensor_tensor(
                out=fold_2[:], in0=att_rows[b][:, :, :HALF], in1=att_rows[b][:, :, HALF:], op=ALU.max
            )

        def fold_again():
            nc.vector.tensor_tensor(out=fold_4[:], in0=fold_2[:, :, :PART], in1=fold_2[:, :, PART:], op=ALU.max)

        def row_max_of_folded(b):
            nc.vector.tensor_reduce(out=neg_max[b][:], in_=fold_4[:], axis=AXIS.X, op=ALU.max, negate=True)

        def exponential(b, lt):
            nc.scalar.activation(
                out=e_rows[b][:, cols(lt, POSITIONS)],
                in_=att_rows[b][:, lt, :],
                func=ACT.Exp,
                bias=neg_max[b][:, lt : lt + 1],
                scale=1.0,
                accum_out=e_sum[b][:, lt : lt + 1],
            )

        def spread_recip(b):
            acc = bank([PART, POSITIONS], F32, "turned")
            for lt in range(L_TILES):
                nc.tensor.transpose(
                    acc[:, cols(lt, PART)], e_recip[b][:, lt : lt + 1].to_broadcast([PART, PART]), ident_f32[:]
                )
            return acc

        def regroup_g_vector(b):
            nc.vector.tensor_copy(
                out=g_by_p[b]["values"][:].rearrange("q (c i t) -> q c t i", i=4, t=PACK),
                in_=g_rows[b][:].rearrange("q (t c i) -> q c t i", t=PACK, i=4),
            )

        def regroup_g_gpsimd(b):
            for piece in range(L_TILES):
                nc.gpsimd.tensor_scalar(
                    out=g_by_p[b]["values"][:, cols(piece, PACK * PART)].rearrange("q (c i t) -> q c t i", i=4, t=PACK),
                    in0=g_rows[b][:].rearrange("q (t m) -> q t m", t=PACK)[:, :, cols(piece, PART)].rearrange(
                        "q t (c i) -> q c t i", i=4
                    ),
                    scalar1=1.0,
                    scalar2=0.0,
                    op0=ALU.mult,
                    op1=ALU.add,
                )

        def aggregate_multiply(b, lt):
            acc = bank([PART, PACK, PART], F32, "y%d" % b)
            for t in range(PACK):
                multiply(acc[:, t, :], g_by_m[b], t, e_by_m[b], lt, PART, True, True)
            return acc

        def aggregate_divide(b, lt, acc):
            nc.vector.tensor_tensor(
                out=y_by_p[b]["values"][:, cols(lt, PACK * PART)].rearrange("q (l t) -> q l t", t=PACK),
                in0=acc[:].rearrange("q t l -> q l t"),
                in1=recip_rows[b][:, cols(lt, PART)].unsqueeze(2).to_broadcast([PART, PART, PACK]),
                op=ALU.mult,
            )

        def project_g(b, ct, piece, width):
            acc = bank([PART, width], F32, "out%d" % b)
            multiply(acc[:], w_by_p[0], ct, g_by_p[b], piece, width, True, False)
            return acc

        def project_y(b, ct, piece, width, acc):
            multiply(acc[:], w_by_p[1], ct, y_by_p[b], piece, width, False, True)

        def leave(b, ct, piece, width, acc, on_vector):
            if on_vector:
                nc.vector.tensor_scalar_add(
                    out=result[b][:, ct, cols(piece, width)], in0=acc[:], scalar1=bias[:, ct : ct + 1]
                )
            else:
                nc.scalar.activation(
                    out=result[b][:, ct, cols(piece, width)],
                    in_=acc[:],
                    func=ACT.Identity,
                    bias=bias[:, ct : ct + 1],
                    scale=1.0,
                )

        def store_piece(b, ct, piece, width):
            out_rows = out[b].rearrange("(i ct) l -> i ct l", ct=C_TILES)
            nc.sync.dma_start(
                out=out_rows[:, ct, cols(piece, width)], in_=result[b][:, ct, cols(piece, width)]
            )

        def store(b, ct, n=2):
            out_rows = out[b].rearrange("(i ct) l -> i ct l", ct=C_TILES)
            nc.sync.dma_start(out=out_rows[:, ct : ct + n, :], in_=result[b][:, ct : ct + n, :])

        def keep_busy(times, width):
            acc = bank([PART, POSITIONS], F32, "unread")
            for i in range(times):
                nc.tensor.matmul(
                    acc[:, :width], lhsT=att_rows[0][:, 0, :PART], rhs=att_rows[0][:, 0, :width], start=True, stop=True
                )

        def project(b, ct, piece, width, on_vector):
            acc = project_g(b, ct, piece, width)
            project_y(b, ct, piece, width, acc)
            leave(b, ct, piece, width, acc, on_vector)
            if ct < 8:
                store(b, ct, 1)
            elif ct % 2 == 1:
                store(b, ct - 1)

        vector_copy, scalar_copy = nc.vector.tensor_copy, nc.scalar.copy
        half_channels = CHANNELS // 2

        keep_busy(4, POSITIONS)

        for lt in range(L_TILES):
            row_max(0, lt)
            exponential(0, lt)
        for pair in range(2):
            turn(g_rows[0], g_by_m[0], pair, scalar_copy)
            keep_busy(1, HALF)
        regroup_g_vector(0)
        nc.vector.reciprocal(out=e_recip[0][:], in_=e_sum[0][:])
        fold_columns(1)
        for pair in range(2):
            turn(e_rows[0], e_by_m[0], pair, scalar_copy)
            keep_busy(1, POSITIONS)
        quantise(g_by_p[0], 0, POSITIONS)
        nc.scalar.copy(out=recip_rows[0][:], in_=spread_recip(0)[:])
        quantise(g_by_m[0], 0, FEATURES)
        quantise(e_by_m[0], 0, 2 * PART)
        fold_again()
        quantise(e_by_m[0], 1, 2 * PART)
        row_max_of_folded(1)

        for pair in range(2):
            turn(w_rows[0], w_by_p[0], pair, scalar_copy)
            keep_busy(1, HALF)
        exponential(1, 0)
        exponential(1, 1)
        y_banks = [aggregate_multiply(0, lt) for lt in range(L_TILES)]
        aggregate_divide(0, 0, y_banks[0])
        turn(w_rows[1], w_by_p[1], 0, scalar_copy)
        turn(w_rows[1], w_by_p[1], 1, scalar_copy)
        regroup_g_gpsimd(1)
        nc.gpsimd.tensor_tensor(out=bias[:], in0=b1[:], in1=b2[:], op=ALU.add)
        for lt in range(1, L_TILES):
            aggregate_divide(0, lt, y_banks[lt])

        for pair in range(2, 4):
            turn(w_rows[0], w_by_p[0], pair, scalar_copy)
        exponential(1, 2)
        exponential(1, 3)
        quantise(w_by_p[0], 0, half_channels)
        quantise(y_by_p[0], 0, POSITIONS)
        g_banks = [transpose_words(g_rows[1], pair) for pair in range(2)]
        e_banks = [transpose_words(e_rows[1], 0, "e1")]
        quantise(w_by_p[1], 0, half_channels)
        turn(w_rows[1], w_by_p[1], 2, scalar_copy)
        first_banks = [project_g(0, ct, 0, POSITIONS) for ct in range(2)]
        for ct in range(2):
            project_y(0, ct, 0, POSITIONS, first_banks[ct])
        for pair in range(2):
            copy_words(g_banks[pair], g_by_m[1], pair, vector_copy)
        copy_words(e_banks[0], e_by_m[1], 0, scalar_copy)
        leave(0, 0, 0, POSITIONS, first_banks[0], False)
        store(0, 0, 1)
        turn(w_rows[1], w_by_p[1], 3, scalar_copy)
        e_banks += [transpose_words(e_rows[1], 1, "e1")]
        nc.vector.reciprocal(out=e_recip[1][:], in_=e_sum[1][:])
        nc.scalar.copy(out=recip_rows[1][:], in_=spread_recip(1)[:])
        quantise(w_by_p[0], 1, half_channels)
        quantise(g_by_m[1], 0, FEATURES)
        copy_words(e_banks[1], e_by_m[1], 1, scalar_copy)
        quantise(e_by_m[1], 0, 2 * PART)
        quantise(g_by_p[1], 0, POSITIONS)
        quantise(w_by_p[1], 1, half_channels)
        leave(0, 1, 0, POSITIONS, first_banks[1], True)
        store(0, 1, 1)
        quantise(e_by_m[1], 1, 2 * PART)
        for ct in range(2, 4):
            project(0, ct, 0, POSITIONS, False)
        y_banks = [aggregate_multiply(1, lt) for lt in range(2)]
        for lt in range(2):
            aggregate_divide(1, lt, y_banks[lt])
        quantise(y_by_p[1], 0, PART)
        for ct in range(4, 6):
            project(0, ct, 0, POSITIONS, False)
        y_banks += [aggregate_multiply(1, lt) for lt in range(2, 4)]
        for ct in range(6, 8):
            project(0, ct, 0, POSITIONS, False)
        for lt in range(2, L_TILES):
            aggregate_divide(1, lt, y_banks[lt])
            quantise(y_by_p[1], lt - 1, PART)
        quantise(y_by_p[1], L_TILES - 1, PART)

        units = [(ct, piece, HALF) for piece in range(2) for ct in range(3)]
        units += [(ct, 0, POSITIONS) for ct in range(3, C_TILES - 1)]
        units += [(ct, piece, HALF) for ct in range(C_TILES - 1, C_TILES) for piece in range(2)]
        ahead = 1
        banks = []
        for i in range(len(units) + ahead):
            if i < len(units):
                ct, piece, width = units[i]
                banks.append(project_g(1, ct, piece, width))
            if i >= ahead:
                ct, piece, width = units[i - ahead]
                project_y(1, ct, piece, width, banks[i - ahead])
                leave(1, ct, piece, width, banks[i - ahead], i % 2 == 1)
                if ct >= C_TILES - 1:
                    store_piece(1, ct, piece, width)
                elif (piece + 1) * width == POSITIONS:
                    store(1, ct, 1)
